import numpy as np
import ml_dtypes


def mxq(x, axis, fmt="e4m3"):
    dtype, down = {"e4m3": (ml_dtypes.float8_e4m3fn, 7), "e5m2": (ml_dtypes.float8_e5m2, 14)}[fmt]
    v = np.moveaxis(np.asarray(x, np.float32).astype(ml_dtypes.bfloat16).astype(np.float64), axis, -1)
    blocks = v.reshape(v.shape[:-1] + (-1, 32))
    amax = np.abs(blocks).max(-1, keepdims=True)
    byte = np.maximum(np.where(amax > 0, np.frexp(amax)[1] - 1 + 127, 0) - down, 1)
    scale = np.exp2(byte - 127.0)
    codes = (blocks / scale).astype(np.float32).astype(dtype).astype(np.float64)
    return np.moveaxis((codes * scale).reshape(v.shape), -1, axis)


WIDE = False


def mx_kscale(k):
    if not WIDE:
        return np.ones(k)
    levels = np.array([10, -10, 5, -5, 0])
    a = np.random.permutation(np.resize(levels, k // 512 * 4)).reshape(k // 512, 4)
    idx = np.arange(k)
    return np.exp2(a[idx // 512, idx % 128 // 32])


BF16 = ml_dtypes.bfloat16


def bf(x):
    return np.asarray(x, np.float32).astype(BF16)


def f64(x):
    return np.asarray(x).astype(np.float64)


B, C, H, W, D, R = 2, 128, 32, 32, 2048, 3
P = R * R
CEN = P // 2
NB = P - 1
PAD = R // 2
KC = NB * C


def neighbours(z):
    zp = np.pad(z, ((0, 0), (0, 0), (PAD, PAD), (PAD, PAD)))
    views = [zp[:, :, di:di + H, dj:dj + W] for di in range(R) for dj in range(R) if di * R + dj != CEN]
    return np.stack(views, axis=2)


def setup_inputs():
    s = mx_kscale(KC)[::NB]
    t = mx_kscale(D)
    return {"z": bf(np.random.standard_normal((B, C, H, W)) * s[None, :, None, None]),
            "W1": bf((np.random.standard_normal((D, C, P)) / np.sqrt(KC) / s[None, :, None] * t[:, None, None]).reshape(D, C * P)),
            "b1": bf(np.random.standard_normal(D) * 0.3 * t),
            "W2": bf(np.random.standard_normal((C, D)) / np.sqrt(D) / t[None, :]),
            "b2": bf(np.random.standard_normal(C) * 0.3)}


def reference(z, W1, b1, W2, b2):
    win = neighbours(f64(z)).transpose(0, 3, 4, 1, 2).reshape(B * H * W, KC)
    w1 = np.delete(f64(W1).reshape(D, C, P), CEN, axis=2).reshape(D, KC)
    h = np.maximum((mxq(win, 1, "e4m3") @ mxq(w1.T, 0, "e4m3")) + f64(b1), 0.0)
    logits = (mxq(h, 1, "e4m3") @ mxq(f64(W2).T, 0, "e4m3")) + f64(b2)
    return logits.reshape(B, H, W, C).transpose(0, 3, 1, 2)

@@ -1,0 +1,294 @@
+from contextlib import ExitStack
+
+import concourse.mybir as mybir
+from concourse.masks import make_identity
+
+BF16 = mybir.dt.bfloat16
+F32 = mybir.dt.float32
+U32 = mybir.dt.uint32
+U8 = mybir.dt.uint8
+FP8X4 = mybir.dt.float8_e4m3fn_x4
+ACT = mybir.ActivationFunctionType
+ALU = mybir.AluOpType
+
+P = 128
+PACK = 4
+K_PASS = P * PACK
+
+BATCH = 2
+CHANNELS = 128
+SIDE = 32
+MAP = SIDE * SIDE
+WINDOW = 9
+HIDDEN = 2048
+
+CHANNEL_PASSES = 2
+PASS_CHANNELS = CHANNELS // CHANNEL_PASSES
+HIDDEN_PASSES = HIDDEN // K_PASS
+PIXEL_TILE = 512
+TILES_PER_MAP = MAP // PIXEL_TILE
+PIXEL_TILES = BATCH * TILES_PER_MAP
+TILE_ROWS = PIXEL_TILE // SIDE
+MARGIN = 64
+RUN = 4
+LAG = 2
+W1_AHEAD = 2
+
+FLOPS = 2 * BATCH * MAP * HIDDEN * (8 * CHANNELS + CHANNELS)
+
+
+def window_position(u, t):
+    return 5 * (t // 2) + 2 * u + t % 2
+
+
+def regroup(nc, grouped, planes):
+    nc.vector.tensor_copy(
+        out=grouped.rearrange("p (x i) t -> p x t i", i=RUN),
+        in_=planes.rearrange("p t (x i) -> p x t i", i=RUN),
+    )
+
+
+def tile_localpredictor_pa_kernel(tc, z, W1, b1, W2, b2, out):
+    nc = tc.nc
+    z_maps = z.rearrange("b c h w -> b c (h w)")
+    out_maps = out.rearrange("b k h w -> b k (h w)")
+    w1_rows = W1.rearrange("(s m t) k -> s m t k", m=P, t=PACK)
+
+    with ExitStack() as ctx:
+        keep = ctx.enter_context(tc.tile_pool(name="keep", bufs=1))
+        w1_pool = ctx.enter_context(tc.tile_pool(name="w1_pool", bufs=2 * HIDDEN_PASSES))
+        stage = ctx.enter_context(tc.tile_pool(name="stage", bufs=4))
+        win_pool = ctx.enter_context(tc.tile_pool(name="win_pool", bufs=2))
+        h_pool = ctx.enter_context(tc.tile_pool(name="h_pool", bufs=LAG + 2))
+        psum = ctx.enter_context(tc.psum_pool(name="psum", bufs=7))
+        psum_out = ctx.enter_context(tc.psum_pool(name="psum_out", bufs=1))
+
+        def load_w1(s):
+            pair_tiles = []
+            for pair in range(2):
+                w1_raw = w1_pool.tile([P, 2, CHANNELS * WINDOW], BF16, name="w1_raw")
+                nc.sync.dma_start(out=w1_raw[:], in_=w1_rows[s, :, 2 * pair : 2 * pair + 2, :])
+                pair_tiles.append(w1_raw)
+            return pair_tiles
+
+        shifted = {}
+        for b in range(BATCH):
+            for g in range(CHANNEL_PASSES):
+                shifted[b, g] = keep.tile([P, PACK, MAP], BF16, name="shifted%d%d" % (b, g))
+                nc.vector.memset(shifted[b, g][:, :, 0:MARGIN], 0.0)
+                nc.vector.memset(shifted[b, g][:, :, MAP - MARGIN : MAP], 0.0)
+
+        def load_shifted(b):
+            for g in range(CHANNEL_PASSES):
+                for u in range(2):
+                    for t in range(PACK):
+                        position = window_position(u, t)
+                        shift = SIDE * (position // 3 - 1) + (position % 3 - 1)
+                        first = max(0, -shift)
+                        last = MAP - max(0, shift)
+                        nc.sync.dma_start(
+                            out=shifted[b, g][u:P:2, t, first:last],
+                            in_=z_maps[b, PASS_CHANNELS * g : PASS_CHANNELS * (g + 1), first + shift : last + shift],
+                        )
+
+        b1_bf16 = keep.tile([P, HIDDEN_PASSES, PACK], BF16, name="b1_bf16")
+        nc.scalar.dma_start(out=b1_bf16[:], in_=b1.rearrange("(s m t) -> m s t", m=P, t=PACK))
+        b2_bf16 = keep.tile([P, 1], BF16, name="b2_bf16")
+        nc.scalar.dma_start(out=b2_bf16[:], in_=b2.rearrange("(k o) -> k o", o=1))
+        w1_raw_tiles = {}
+        for s in range(W1_AHEAD):
+            w1_raw_tiles[s] = load_w1(s)
+        load_shifted(0)
+        w2_rows = keep.tile([P, HIDDEN], BF16, name="w2_rows")
+        nc.sync.dma_start(out=w2_rows[:], in_=W2)
+        for s in range(W1_AHEAD, HIDDEN_PASSES):
+            w1_raw_tiles[s] = load_w1(s)
+        load_shifted(1)
+
+        identity = keep.tile([P, P], F32, name="identity")
+        make_identity(nc, identity[:])
+        bias1 = keep.tile([P, HIDDEN_PASSES, PACK], F32, name="bias1")
+        nc.vector.tensor_copy(out=bias1[:], in_=b1_bf16[:])
+        bias2 = keep.tile([P, 1], F32, name="bias2")
+        nc.vector.tensor_copy(out=bias2[:], in_=b2_bf16[:])
+
+        odd = keep.tile([P, 1], F32, name="odd")
+        nc.vector.tensor_reduce(out=odd[:], in_=identity[:, 1:P:2], axis=mybir.AxisListType.X, op=ALU.add)
+        even = keep.tile([P, 1], F32, name="even")
+        nc.vector.tensor_scalar(out=even[:], in0=odd[:], scalar1=-1.0, scalar2=1.0, op0=ALU.mult, op1=ALU.add)
+        edge = keep.tile([P, 2, PACK], BF16, name="edge")
+        nc.vector.memset(edge[:], 1.0)
+        for side, missing_column in enumerate((0, 2)):
+            for t in range(PACK):
+                for u, other_parity in ((0, odd), (1, even)):
+                    if window_position(u, t) % 3 == missing_column:
+                        nc.vector.tensor_copy(out=edge[:, side, t : t + 1], in_=other_parity[:])
+
+        w1_codes = keep.tile([P, 2 * HIDDEN_PASSES, CHANNEL_PASSES, 2 * P], U32, name="w1_codes", align_bytes=64)
+        w1_scales = keep.tile([P, 2 * HIDDEN_PASSES, CHANNEL_PASSES, 2 * P], U8, name="w1_scales", align_bytes=64)
+
+        def compact_w1(s):
+            compacted = []
+            for w1_raw in w1_raw_tiles[s]:
+                halves = stage.tile([P, 2, 2, K_PASS], BF16, name="halves")
+                by_channel = w1_raw[:].rearrange("m j (c x) -> m j c x", x=WINDOW)
+                for a in range(2):
+                    nc.vector.tensor_copy(
+                        out=halves[:, a].rearrange("m j (c r) -> m j c r", r=PACK),
+                        in_=by_channel[:, :, :, 5 * a : 5 * a + PACK],
+                    )
+                compacted.append(halves)
+            return compacted
+
+        def transpose_w1(compacted):
+            grouped_tiles = []
+            for halves in compacted:
+                words = halves[:].bitcast(F32)
+                w1_grouped = stage.tile([P, CHANNEL_PASSES, 2 * P, 2], F32, name="w1_grouped", align_bytes=64)
+                for g in range(CHANNEL_PASSES):
+                    bank = psum.tile([P, 2, 2, P], F32, tag="bank")
+                    for a in range(2):
+                        for j in range(2):
+                            nc.tensor.transpose(bank[:, a, j, :], words[:, a, j, P * g : P * (g + 1)], identity[:])
+                    nc.scalar.copy(out=w1_grouped[:, g], in_=bank[:].rearrange("p a j m -> p (j m) a"))
+                grouped_tiles.append(w1_grouped)
+            return grouped_tiles
+
+        def quantise_w1(s, grouped_tiles):
+            for pair, w1_grouped in enumerate(grouped_tiles):
+                q = 2 * s + pair
+                nc.vector.quantize_mx(
+                    out=w1_codes[:, q].rearrange("p g m -> p (g m)").bitcast(FP8X4),
+                    scales=w1_scales[:, q].rearrange("p g m -> p (g m)"),
+                    in_=w1_grouped[:].rearrange("p g m a -> p (g m a)").bitcast(BF16),
+                )
+
+        w2_codes = keep.tile([P, HIDDEN_PASSES, P], U32, name="w2_codes", align_bytes=64)
+        w2_scales = keep.tile([P, HIDDEN_PASSES, P], U8, name="w2_scales", align_bytes=64)
+
+        def prepare_w2():
+            words = w2_rows[:].bitcast(F32)
+            w2_grouped = keep.tile([P, HIDDEN_PASSES * P, 2], F32, name="w2_grouped", align_bytes=64)
+            for pair in range(HIDDEN_PASSES // 2):
+                bank = psum.tile([P, 2, 2, P], F32, tag="bank")
+                for u in range(2):
+                    for j in range(2):
+                        s = 2 * pair + j
+                        nc.tensor.transpose(bank[:, u, j, :], words[:, 2 * P * s + u : 2 * P * (s + 1) : 2], identity[:])
+                nc.scalar.copy(
+                    out=w2_grouped[:, 2 * P * pair : 2 * P * (pair + 1), :],
+                    in_=bank[:].rearrange("p u j k -> p (j k) u"),
+                )
+            nc.vector.quantize_mx(
+                out=w2_codes[:].rearrange("p s k -> p (s k)").bitcast(FP8X4),
+                scales=w2_scales[:].rearrange("p s k -> p (s k)"),
+                in_=w2_grouped[:].rearrange("p k u -> p (k u)").bitcast(BF16),
+            )
+
+        def gather_windows(n):
+            b, half = divmod(n, TILES_PER_MAP)
+            win_grouped = win_pool.tile([P, CHANNEL_PASSES, PIXEL_TILE, PACK], BF16, name="win_grouped", align_bytes=64)
+            for g in range(CHANNEL_PASSES):
+                regroup(nc, win_grouped[:, g], shifted[b, g][:, :, PIXEL_TILE * half : PIXEL_TILE * (half + 1)])
+            row_ends = win_grouped[:].rearrange("p g (i j) t -> p (g i) j t", j=SIDE)[:, :, 0 : SIDE : SIDE - 1, :]
+            nc.vector.tensor_tensor(
+                out=row_ends,
+                in0=row_ends,
+                in1=edge[:].unsqueeze(1).to_broadcast([P, CHANNEL_PASSES * TILE_ROWS, 2, PACK]),
+                op=ALU.mult,
+            )
+            return win_grouped
+
+        def quantise_windows(win_grouped):
+            win_codes = win_pool.tile([P, CHANNEL_PASSES, PIXEL_TILE], U32, name="win_codes", align_bytes=64)
+            win_scales = win_pool.tile([P, CHANNEL_PASSES, PIXEL_TILE], U8, name="win_scales", align_bytes=64)
+            nc.vector.quantize_mx(
+                out=win_codes[:].rearrange("p g x -> p (g x)").bitcast(FP8X4),
+                scales=win_scales[:].rearrange("p g x -> p (g x)"),
+                in_=win_grouped[:].rearrange("p g x t -> p (g x t)"),
+            )
+            return win_codes, win_scales
+
+        def first_layer(s, win_codes, win_scales):
+            hidden = h_pool.tile([P, PACK, PIXEL_TILE], BF16, name="hidden")
+            for t in range(PACK):
+                q, j = 2 * s + t // 2, t % 2
+                bank = psum.tile([P, PIXEL_TILE], F32, tag="bank")
+                for g in range(CHANNEL_PASSES):
+                    nc.tensor.matmul_mx(
+                        out=bank[:],
+                        lhsT=w1_codes[:, q, g, P * j : P * (j + 1)].bitcast(FP8X4),
+                        lhsT_scale=w1_scales[:, q, g, P * j : P * (j + 1)],
+                        rhs=win_codes[:, g, :].bitcast(FP8X4),
+                        rhs_scale=win_scales[:, g, :],
+                        start=(g == 0),
+                        stop=(g == CHANNEL_PASSES - 1),
+                    )
+                nc.scalar.activation(out=hidden[:, t, :], in_=bank[:], func=ACT.Relu, bias=bias1[:, s, t : t + 1])
+            return hidden
+
+        def regroup_hidden(hidden):
+            h_grouped = h_pool.tile([P, PIXEL_TILE, PACK], BF16, name="h_grouped", align_bytes=64)
+            regroup(nc, h_grouped[:], hidden[:])
+            return h_grouped
+
+        def quantise_hidden(h_grouped):
+            h_codes = h_pool.tile([P, PIXEL_TILE], U32, name="h_codes", align_bytes=64)
+            h_scales = h_pool.tile([P, PIXEL_TILE], U8, name="h_scales", align_bytes=64)
+            nc.vector.quantize_mx(
+                out=h_codes[:].bitcast(FP8X4),
+                scales=h_scales[:],
+                in_=h_grouped[:].rearrange("p x t -> p (x t)"),
+            )
+            return h_codes, h_scales
+
+        out_banks = {}
+
+        def second_layer(n, s, h_codes, h_scales):
+            if s == 0:
+                out_banks[n] = psum_out.tile([P, PIXEL_TILE], F32, name="out_bank")
+            nc.tensor.matmul_mx(
+                out=out_banks[n][:],
+                lhsT=w2_codes[:, s, :].bitcast(FP8X4),
+                lhsT_scale=w2_scales[:, s, :],
+                rhs=h_codes[:].bitcast(FP8X4),
+                rhs_scale=h_scales[:],
+                start=(s == 0),
+                stop=(s == HIDDEN_PASSES - 1),
+            )
+            if s == HIDDEN_PASSES - 1:
+                b, half = divmod(n, TILES_PER_MAP)
+                result = stage.tile([P, PIXEL_TILE], F32, name="result")
+                nc.scalar.activation(out=result[:], in_=out_banks[n][:], func=ACT.Identity, bias=bias2[:, 0:1])
+                nc.sync.dma_start(out=out_maps[b, :, PIXEL_TILE * half : PIXEL_TILE * (half + 1)], in_=result[:])
+
+        for s in range(W1_AHEAD):
+            quantise_w1(s, transpose_w1(compact_w1(s)))
+        win_operands = {0: quantise_windows(gather_windows(0))}
+        windows = {}
+        prepare_w2()
+
+        blocks = [(n, s) for n in range(PIXEL_TILES) for s in range(HIDDEN_PASSES)]
+        grouped_blocks = {}
+        quantised_blocks = {}
+        for i in range(len(blocks) + LAG):
+            if i < len(blocks):
+                n, s = blocks[i]
+                prepare_next_w1 = n == 0 and s + W1_AHEAD < HIDDEN_PASSES
+                if prepare_next_w1:
+                    compacted = compact_w1(s + W1_AHEAD)
+                hidden = first_layer(s, win_operands[n][0], win_operands[n][1])
+                if prepare_next_w1:
+                    w1_grouped_tiles = transpose_w1(compacted)
+                if s == 1 and n + 1 < PIXEL_TILES:
+                    windows[n + 1] = gather_windows(n + 1)
+                grouped_blocks[i] = regroup_hidden(hidden)
+                if s == 2 and n + 1 < PIXEL_TILES:
+                    win_operands[n + 1] = quantise_windows(windows[n + 1])
+                if prepare_next_w1:
+                    quantise_w1(s + W1_AHEAD, w1_grouped_tiles)
+            if 0 <= i - 1 < len(blocks):
+                quantised_blocks[i - 1] = quantise_hidden(grouped_blocks[i - 1])
+            if i >= LAG:
+                n, s = blocks[i - LAG]
+                second_layer(n, s, quantised_blocks[i - LAG][0], quantised_blocks[i - LAG][1])

@@ -31,7 +31,7 @@ PIXEL_TILES = BATCH * TILES_PER_MAP
 TILE_ROWS = PIXEL_TILE // SIDE
 MARGIN = 64
 RUN = 4
-LAG = 2
+REGROUP_LAG = 2
 W1_AHEAD = 2
 
 FLOPS = 2 * BATCH * MAP * HIDDEN * (8 * CHANNELS + CHANNELS)
@@ -55,11 +55,12 @@ def tile_localpredictor_pa_kernel(tc, z, W1, b1, W2, b2, out):
     w1_rows = W1.rearrange("(s m t) k -> s m t k", m=P, t=PACK)
 
     with ExitStack() as ctx:
+        ctx.enter_context(tc.manual_schedule())
         keep = ctx.enter_context(tc.tile_pool(name="keep", bufs=1))
         w1_pool = ctx.enter_context(tc.tile_pool(name="w1_pool", bufs=2 * HIDDEN_PASSES))
         stage = ctx.enter_context(tc.tile_pool(name="stage", bufs=4))
         win_pool = ctx.enter_context(tc.tile_pool(name="win_pool", bufs=2))
-        h_pool = ctx.enter_context(tc.tile_pool(name="h_pool", bufs=LAG + 2))
+        h_pool = ctx.enter_context(tc.tile_pool(name="h_pool", bufs=REGROUP_LAG + 2))
         psum = ctx.enter_context(tc.psum_pool(name="psum", bufs=7))
         psum_out = ctx.enter_context(tc.psum_pool(name="psum_out", bufs=1))
 
@@ -108,21 +109,22 @@ def tile_localpredictor_pa_kernel(tc, z, W1, b1, W2, b2, out):
         identity = keep.tile([P, P], F32, name="identity")
         make_identity(nc, identity[:])
         bias1 = keep.tile([P, HIDDEN_PASSES, PACK], F32, name="bias1")
-        nc.vector.tensor_copy(out=bias1[:], in_=b1_bf16[:])
         bias2 = keep.tile([P, 1], F32, name="bias2")
-        nc.vector.tensor_copy(out=bias2[:], in_=b2_bf16[:])
-
         odd = keep.tile([P, 1], F32, name="odd")
-        nc.vector.tensor_reduce(out=odd[:], in_=identity[:, 1:P:2], axis=mybir.AxisListType.X, op=ALU.add)
         even = keep.tile([P, 1], F32, name="even")
-        nc.vector.tensor_scalar(out=even[:], in0=odd[:], scalar1=-1.0, scalar2=1.0, op0=ALU.mult, op1=ALU.add)
         edge = keep.tile([P, 2, PACK], BF16, name="edge")
-        nc.vector.memset(edge[:], 1.0)
-        for side, missing_column in enumerate((0, 2)):
-            for t in range(PACK):
-                for u, other_parity in ((0, odd), (1, even)):
-                    if window_position(u, t) % 3 == missing_column:
-                        nc.vector.tensor_copy(out=edge[:, side, t : t + 1], in_=other_parity[:])
+
+        def prepare_small_operands():
+            nc.vector.tensor_copy(out=bias1[:], in_=b1_bf16[:])
+            nc.vector.tensor_copy(out=bias2[:], in_=b2_bf16[:])
+            nc.vector.tensor_reduce(out=odd[:], in_=identity[:, 1:P:2], axis=mybir.AxisListType.X, op=ALU.add)
+            nc.vector.tensor_scalar(out=even[:], in0=odd[:], scalar1=-1.0, scalar2=1.0, op0=ALU.mult, op1=ALU.add)
+            nc.vector.memset(edge[:], 1.0)
+            for side, missing_column in enumerate((0, 2)):
+                for t in range(PACK):
+                    for u, other_parity in ((0, odd), (1, even)):
+                        if window_position(u, t) % 3 == missing_column:
+                            nc.vector.tensor_copy(out=edge[:, side, t : t + 1], in_=other_parity[:])
 
         w1_codes = keep.tile([P, 2 * HIDDEN_PASSES, CHANNEL_PASSES, 2 * P], U32, name="w1_codes", align_bytes=64)
         w1_scales = keep.tile([P, 2 * HIDDEN_PASSES, CHANNEL_PASSES, 2 * P], U8, name="w1_scales", align_bytes=64)
@@ -262,33 +264,46 @@ def tile_localpredictor_pa_kernel(tc, z, W1, b1, W2, b2, out):
                 nc.scalar.activation(out=result[:], in_=out_banks[n][:], func=ACT.Identity, bias=bias2[:, 0:1])
                 nc.sync.dma_start(out=out_maps[b, :, PIXEL_TILE * half : PIXEL_TILE * (half + 1)], in_=result[:])
 
+        compacted = compact_w1(0)
+        prepare_small_operands()
         for s in range(W1_AHEAD):
-            quantise_w1(s, transpose_w1(compact_w1(s)))
-        win_operands = {0: quantise_windows(gather_windows(0))}
-        windows = {}
+            w1_grouped_tiles = transpose_w1(compacted)
+            if s + 1 < W1_AHEAD:
+                compacted = compact_w1(s + 1)
+            else:
+                windows = {0: gather_windows(0)}
+            quantise_w1(s, w1_grouped_tiles)
+        win_operands = {0: quantise_windows(windows[0])}
         prepare_w2()
 
         blocks = [(n, s) for n in range(PIXEL_TILES) for s in range(HIDDEN_PASSES)]
+        hidden_blocks = {}
         grouped_blocks = {}
         quantised_blocks = {}
-        for i in range(len(blocks) + LAG):
-            if i < len(blocks):
+        for i in range(len(blocks) + REGROUP_LAG + 2):
+            in_first_layer = i < len(blocks)
+            prepare_next_w1 = in_first_layer and i + W1_AHEAD < HIDDEN_PASSES
+            if in_first_layer:
                 n, s = blocks[i]
-                prepare_next_w1 = n == 0 and s + W1_AHEAD < HIDDEN_PASSES
                 if prepare_next_w1:
                     compacted = compact_w1(s + W1_AHEAD)
-                hidden = first_layer(s, win_operands[n][0], win_operands[n][1])
+                hidden_blocks[i] = first_layer(s, win_operands[n][0], win_operands[n][1])
                 if prepare_next_w1:
                     w1_grouped_tiles = transpose_w1(compacted)
-                if s == 1 and n + 1 < PIXEL_TILES:
+            to_regroup = i - REGROUP_LAG
+            if 0 <= to_regroup < len(blocks):
+                grouped_blocks[to_regroup] = regroup_hidden(hidden_blocks[to_regroup])
+            to_quantise = to_regroup - 1
+            if 0 <= to_quantise < len(blocks):
+                quantised_blocks[to_quantise] = quantise_hidden(grouped_blocks[to_quantise])
+            if in_first_layer and n + 1 < PIXEL_TILES:
+                if s == 0:
                     windows[n + 1] = gather_windows(n + 1)
-                grouped_blocks[i] = regroup_hidden(hidden)
-                if s == 2 and n + 1 < PIXEL_TILES:
+                if s == 1:
                     win_operands[n + 1] = quantise_windows(windows[n + 1])
-                if prepare_next_w1:
-                    quantise_w1(s + W1_AHEAD, w1_grouped_tiles)
-            if 0 <= i - 1 < len(blocks):
-                quantised_blocks[i - 1] = quantise_hidden(grouped_blocks[i - 1])
-            if i >= LAG:
-                n, s = blocks[i - LAG]
-                second_layer(n, s, quantised_blocks[i - LAG][0], quantised_blocks[i - LAG][1])
+            if prepare_next_w1:
+                quantise_w1(s + W1_AHEAD, w1_grouped_tiles)
+            to_multiply = to_quantise - 1
+            if to_multiply >= 0:
+                n2, s2 = blocks[to_multiply]
+                second_layer(n2, s2, quantised_blocks[to_multiply][0], quantised_blocks[to_multiply][1])

@@ -32,7 +32,7 @@ TILE_ROWS = PIXEL_TILE // SIDE
 MARGIN = 64
 RUN = 4
 REGROUP_LAG = 2
-W1_AHEAD = 2
+W1_AHEAD = 3
 
 FLOPS = 2 * BATCH * MAP * HIDDEN * (8 * CHANNELS + CHANNELS)
 

@@ -29,16 +29,34 @@ PIXEL_TILE = 512
 TILES_PER_MAP = MAP // PIXEL_TILE
 PIXEL_TILES = BATCH * TILES_PER_MAP
 TILE_ROWS = PIXEL_TILE // SIDE
-MARGIN = 64
+PITCH = SIDE + 1
+BASE = PITCH + 1
+PADDED = BASE + SIDE * PITCH + BASE
+LOADED_FIRST = 2
 RUN = 4
-REGROUP_LAG = 2
-W1_AHEAD = 3
+HIDDEN_BUFS = 6
+COMPACTED_BY_SCALAR = (2,)
+OUTPUT_LAG = 9
+QUANT_LAG = 3
+GATHER_STEP = 1
+FIRST_GATHER = 3
+MAP_STEP = 6
+SPREAD = 1
+W2_STEP = 5
+REGROUP_LAG = 3
+PAIRS = 2 * HIDDEN_PASSES
+PAIRS_AHEAD = 4
 
 FLOPS = 2 * BATCH * MAP * HIDDEN * (8 * CHANNELS + CHANNELS)
 
 
 def window_position(u, t):
     return 5 * (t // 2) + 2 * u + t % 2
+
+
+def pixel_shift(u, t):
+    position = window_position(u, t)
+    return PITCH * (position // 3 - 1) + (position % 3 - 1)
 
 
 def regroup(nc, grouped, planes):
@@ -57,113 +75,114 @@ def tile_localpredictor_pa_kernel(tc, z, W1, b1, W2, b2, out):
     with ExitStack() as ctx:
         ctx.enter_context(tc.manual_schedule())
         keep = ctx.enter_context(tc.tile_pool(name="keep", bufs=1))
-        w1_pool = ctx.enter_context(tc.tile_pool(name="w1_pool", bufs=2 * HIDDEN_PASSES))
+        w1_pool = ctx.enter_context(tc.tile_pool(name="w1_pool", bufs=PAIRS))
         stage = ctx.enter_context(tc.tile_pool(name="stage", bufs=4))
+        shift_pool = ctx.enter_context(tc.tile_pool(name="shift_pool", bufs=2 * CHANNEL_PASSES))
         win_pool = ctx.enter_context(tc.tile_pool(name="win_pool", bufs=2))
-        h_pool = ctx.enter_context(tc.tile_pool(name="h_pool", bufs=REGROUP_LAG + 2))
+        h_pool = ctx.enter_context(tc.tile_pool(name="h_pool", bufs=5))
         psum = ctx.enter_context(tc.psum_pool(name="psum", bufs=7))
         psum_out = ctx.enter_context(tc.psum_pool(name="psum_out", bufs=1))
 
-        def load_w1(s):
-            pair_tiles = []
-            for pair in range(2):
-                w1_raw = w1_pool.tile([P, 2, CHANNELS * WINDOW], BF16, name="w1_raw")
-                nc.sync.dma_start(out=w1_raw[:], in_=w1_rows[s, :, 2 * pair : 2 * pair + 2, :])
-                pair_tiles.append(w1_raw)
-            return pair_tiles
-
-        shifted = {}
-        for b in range(BATCH):
-            for g in range(CHANNEL_PASSES):
-                shifted[b, g] = keep.tile([P, PACK, MAP], BF16, name="shifted%d%d" % (b, g))
-                nc.vector.memset(shifted[b, g][:, :, 0:MARGIN], 0.0)
-                nc.vector.memset(shifted[b, g][:, :, MAP - MARGIN : MAP], 0.0)
-
-        def load_shifted(b):
-            for g in range(CHANNEL_PASSES):
-                for u in range(2):
-                    for t in range(PACK):
-                        position = window_position(u, t)
-                        shift = SIDE * (position // 3 - 1) + (position % 3 - 1)
-                        first = max(0, -shift)
-                        last = MAP - max(0, shift)
-                        nc.sync.dma_start(
-                            out=shifted[b, g][u:P:2, t, first:last],
-                            in_=z_maps[b, PASS_CHANNELS * g : PASS_CHANNELS * (g + 1), first + shift : last + shift],
-                        )
-
-        b1_bf16 = keep.tile([P, HIDDEN_PASSES, PACK], BF16, name="b1_bf16")
-        nc.scalar.dma_start(out=b1_bf16[:], in_=b1.rearrange("(s m t) -> m s t", m=P, t=PACK))
-        b2_bf16 = keep.tile([P, 1], BF16, name="b2_bf16")
-        nc.scalar.dma_start(out=b2_bf16[:], in_=b2.rearrange("(k o) -> k o", o=1))
-        w1_raw_tiles = {}
-        for s in range(W1_AHEAD):
-            w1_raw_tiles[s] = load_w1(s)
-        load_shifted(0)
-        w2_rows = keep.tile([P, HIDDEN], BF16, name="w2_rows")
-        nc.sync.dma_start(out=w2_rows[:], in_=W2)
-        for s in range(W1_AHEAD, HIDDEN_PASSES):
-            w1_raw_tiles[s] = load_w1(s)
-        load_shifted(1)
-
         identity = keep.tile([P, P], F32, name="identity")
         make_identity(nc, identity[:])
-        bias1 = keep.tile([P, HIDDEN_PASSES, PACK], F32, name="bias1")
-        bias2 = keep.tile([P, 1], F32, name="bias2")
-        odd = keep.tile([P, 1], F32, name="odd")
-        even = keep.tile([P, 1], F32, name="even")
-        edge = keep.tile([P, 2, PACK], BF16, name="edge")
 
-        def prepare_small_operands():
-            nc.vector.tensor_copy(out=bias1[:], in_=b1_bf16[:])
-            nc.vector.tensor_copy(out=bias2[:], in_=b2_bf16[:])
-            nc.vector.tensor_reduce(out=odd[:], in_=identity[:, 1:P:2], axis=mybir.AxisListType.X, op=ALU.add)
-            nc.vector.tensor_scalar(out=even[:], in0=odd[:], scalar1=-1.0, scalar2=1.0, op0=ALU.mult, op1=ALU.add)
-            nc.vector.memset(edge[:], 1.0)
-            for side, missing_column in enumerate((0, 2)):
-                for t in range(PACK):
-                    for u, other_parity in ((0, odd), (1, even)):
-                        if window_position(u, t) % 3 == missing_column:
-                            nc.vector.tensor_copy(out=edge[:, side, t : t + 1], in_=other_parity[:])
+        w1_raw_tiles = {}
+
+        def load_w1(q):
+            w1_raw = w1_pool.tile([P, 2, CHANNELS * WINDOW], BF16, name="w1_raw")
+            s, pair = divmod(q, 2)
+            nc.sync.dma_start(out=w1_raw[:], in_=w1_rows[s, :, 2 * pair : 2 * pair + 2, :])
+            w1_raw_tiles[q] = w1_raw
+
+        padded = {}
+        for b in range(BATCH):
+            padded[b] = keep.tile([P, PACK, PADDED], BF16, name="padded%d" % b)
+            nc.gpsimd.memset(padded[b][:].rearrange("c t f -> c (t f)").bitcast(U32), 0)
+        z_rows = {}
+
+        def load_map(b):
+            z_rows[b] = keep.tile([P, SIDE, SIDE], BF16, name="z_rows%d" % b)
+            nc.sync.dma_start(out=z_rows[b][:].rearrange("c i j -> c (i j)"), in_=z_maps[b])
+
+        def pad_map(b):
+            for t in range(PACK):
+                first = BASE - pixel_shift(0, t)
+                rows = padded[b][:, t, first : first + SIDE * PITCH].rearrange("c (i j) -> c i j", j=PITCH)
+                copy = nc.scalar.copy if t in (0, 3) else nc.vector.tensor_copy
+                copy(out=rows[:, :, 0:SIDE], in_=z_rows[b][:])
+
+        shifted = {}
+
+        def load_shifted(n, g):
+            b, half = divmod(n, TILES_PER_MAP)
+            shifted[n, g] = shift_pool.tile([P, PACK, TILE_ROWS * PITCH], BF16, name="shifted_maps")
+            first = BASE + TILE_ROWS * PITCH * half
+            channels = slice(PASS_CHANNELS * g, PASS_CHANNELS * (g + 1))
+            nc.sync.dma_start(
+                out=shifted[n, g][0:P:2, :, :],
+                in_=padded[b][channels, :, first : first + TILE_ROWS * PITCH],
+            )
+            for values in (slice(0, PACK, 3), slice(1, 3)):
+                step = pixel_shift(1, values.start) - pixel_shift(0, values.start)
+                nc.sync.dma_start(
+                    out=shifted[n, g][1:P:2, values, :],
+                    in_=padded[b][channels, values, first + step : first + step + TILE_ROWS * PITCH],
+                )
+
+        bias1 = keep.tile([P, HIDDEN_PASSES, PACK], BF16, name="bias1")
+        nc.scalar.dma_start(out=bias1[:], in_=b1.rearrange("(s m t) -> m s t", m=P, t=PACK))
+        bias2 = keep.tile([P, 1], BF16, name="bias2")
+        nc.scalar.dma_start(out=bias2[:], in_=b2.rearrange("(k o) -> k o", o=1))
+        load_map(0)
+        for q in range(LOADED_FIRST):
+            load_w1(q)
+        pad_map(0)
+        for g in range(CHANNEL_PASSES):
+            load_shifted(0, g)
+        for q in range(LOADED_FIRST, PAIRS):
+            load_w1(q)
+        for g in range(CHANNEL_PASSES):
+            load_shifted(1, g)
+        w2_rows = keep.tile([P, HIDDEN], BF16, name="w2_rows")
+        nc.sync.dma_start(out=w2_rows[:], in_=W2)
+        load_map(1)
+
+        def load_second_map():
+            pad_map(1)
+            for n in range(TILES_PER_MAP, PIXEL_TILES):
+                for g in range(CHANNEL_PASSES):
+                    load_shifted(n, g)
 
         w1_codes = keep.tile([P, 2 * HIDDEN_PASSES, CHANNEL_PASSES, 2 * P], U32, name="w1_codes", align_bytes=64)
         w1_scales = keep.tile([P, 2 * HIDDEN_PASSES, CHANNEL_PASSES, 2 * P], U8, name="w1_scales", align_bytes=64)
 
-        def compact_w1(s):
-            compacted = []
-            for w1_raw in w1_raw_tiles[s]:
-                halves = stage.tile([P, 2, 2, K_PASS], BF16, name="halves")
-                by_channel = w1_raw[:].rearrange("m j (c x) -> m j c x", x=WINDOW)
-                for a in range(2):
-                    nc.vector.tensor_copy(
-                        out=halves[:, a].rearrange("m j (c r) -> m j c r", r=PACK),
-                        in_=by_channel[:, :, :, 5 * a : 5 * a + PACK],
-                    )
-                compacted.append(halves)
-            return compacted
-
-        def transpose_w1(compacted):
-            grouped_tiles = []
-            for halves in compacted:
-                words = halves[:].bitcast(F32)
-                w1_grouped = stage.tile([P, CHANNEL_PASSES, 2 * P, 2], F32, name="w1_grouped", align_bytes=64)
-                for g in range(CHANNEL_PASSES):
-                    bank = psum.tile([P, 2, 2, P], F32, tag="bank")
-                    for a in range(2):
-                        for j in range(2):
-                            nc.tensor.transpose(bank[:, a, j, :], words[:, a, j, P * g : P * (g + 1)], identity[:])
-                    nc.scalar.copy(out=w1_grouped[:, g], in_=bank[:].rearrange("p a j m -> p (j m) a"))
-                grouped_tiles.append(w1_grouped)
-            return grouped_tiles
-
-        def quantise_w1(s, grouped_tiles):
-            for pair, w1_grouped in enumerate(grouped_tiles):
-                q = 2 * s + pair
-                nc.vector.quantize_mx(
-                    out=w1_codes[:, q].rearrange("p g m -> p (g m)").bitcast(FP8X4),
-                    scales=w1_scales[:, q].rearrange("p g m -> p (g m)"),
-                    in_=w1_grouped[:].rearrange("p g m a -> p (g m a)").bitcast(BF16),
+        def compact_w1(q, copy):
+            halves = stage.tile([P, 2, 2, K_PASS], BF16, name="halves")
+            by_channel = w1_raw_tiles[q][:].rearrange("m j (c x) -> m j c x", x=WINDOW)
+            for a in range(2):
+                copy(
+                    out=halves[:, a].rearrange("m j (c r) -> m j c r", r=PACK),
+                    in_=by_channel[:, :, :, 5 * a : 5 * a + PACK],
                 )
+            return halves
+
+        def transpose_w1(halves):
+            words = halves[:].bitcast(F32)
+            w1_grouped = stage.tile([P, CHANNEL_PASSES, 2 * P, 2], F32, name="w1_grouped", align_bytes=64)
+            for g in range(CHANNEL_PASSES):
+                bank = psum.tile([P, 2, 2, P], F32, tag="bank")
+                for a in range(2):
+                    for j in range(2):
+                        nc.tensor.transpose(bank[:, a, j, :], words[:, a, j, P * g : P * (g + 1)], identity[:])
+                nc.scalar.copy(out=w1_grouped[:, g], in_=bank[:].rearrange("p a j m -> p (j m) a"))
+            return w1_grouped
+
+        def quantise_w1(q, w1_grouped):
+            nc.vector.quantize_mx(
+                out=w1_codes[:, q].rearrange("p g m -> p (g m)").bitcast(FP8X4),
+                scales=w1_scales[:, q].rearrange("p g m -> p (g m)"),
+                in_=w1_grouped[:].rearrange("p g m a -> p (g m a)").bitcast(BF16),
+            )
 
         w2_codes = keep.tile([P, HIDDEN_PASSES, P], U32, name="w2_codes", align_bytes=64)
         w2_scales = keep.tile([P, HIDDEN_PASSES, P], U8, name="w2_scales", align_bytes=64)
@@ -187,50 +206,60 @@ def tile_localpredictor_pa_kernel(tc, z, W1, b1, W2, b2, out):
                 in_=w2_grouped[:].rearrange("p k u -> p (k u)").bitcast(BF16),
             )
 
-        def gather_windows(n):
-            b, half = divmod(n, TILES_PER_MAP)
-            win_grouped = win_pool.tile([P, CHANNEL_PASSES, PIXEL_TILE, PACK], BF16, name="win_grouped", align_bytes=64)
-            for g in range(CHANNEL_PASSES):
-                regroup(nc, win_grouped[:, g], shifted[b, g][:, :, PIXEL_TILE * half : PIXEL_TILE * (half + 1)])
-            row_ends = win_grouped[:].rearrange("p g (i j) t -> p (g i) j t", j=SIDE)[:, :, 0 : SIDE : SIDE - 1, :]
-            nc.vector.tensor_tensor(
-                out=row_ends,
-                in0=row_ends,
-                in1=edge[:].unsqueeze(1).to_broadcast([P, CHANNEL_PASSES * TILE_ROWS, 2, PACK]),
-                op=ALU.mult,
-            )
-            return win_grouped
+        win_operands = {}
 
-        def quantise_windows(win_grouped):
+        def start_windows(n):
+            win_grouped = win_pool.tile([P, CHANNEL_PASSES, PIXEL_TILE, PACK], BF16, name="win_grouped", align_bytes=64)
             win_codes = win_pool.tile([P, CHANNEL_PASSES, PIXEL_TILE], U32, name="win_codes", align_bytes=64)
             win_scales = win_pool.tile([P, CHANNEL_PASSES, PIXEL_TILE], U8, name="win_scales", align_bytes=64)
-            nc.vector.quantize_mx(
-                out=win_codes[:].rearrange("p g x -> p (g x)").bitcast(FP8X4),
-                scales=win_scales[:].rearrange("p g x -> p (g x)"),
-                in_=win_grouped[:].rearrange("p g x t -> p (g x t)"),
-            )
-            return win_codes, win_scales
+            win_operands[n] = (win_codes, win_scales)
+            return win_grouped
 
-        def first_layer(s, win_codes, win_scales):
-            hidden = h_pool.tile([P, PACK, PIXEL_TILE], BF16, name="hidden")
-            for t in range(PACK):
-                q, j = 2 * s + t // 2, t % 2
-                bank = psum.tile([P, PIXEL_TILE], F32, tag="bank")
-                for g in range(CHANNEL_PASSES):
-                    nc.tensor.matmul_mx(
-                        out=bank[:],
-                        lhsT=w1_codes[:, q, g, P * j : P * (j + 1)].bitcast(FP8X4),
-                        lhsT_scale=w1_scales[:, q, g, P * j : P * (j + 1)],
-                        rhs=win_codes[:, g, :].bitcast(FP8X4),
-                        rhs_scale=win_scales[:, g, :],
-                        start=(g == 0),
-                        stop=(g == CHANNEL_PASSES - 1),
+        def gather_windows(n, g, win_grouped):
+            rows = shifted[n, g][:].rearrange("p t (r j) -> p t r j", j=PITCH)[:, :, :, 0:SIDE]
+            nc.vector.tensor_copy(
+                out=win_grouped[:, g].rearrange("p (r x i) t -> p r x t i", r=TILE_ROWS, i=RUN),
+                in_=rows.rearrange("p t r (x i) -> p r x t i", i=RUN),
+            )
+
+        def quantise_windows(n, g_first, g_end, win_grouped):
+            win_codes, win_scales = win_operands[n]
+            nc.vector.quantize_mx(
+                out=win_codes[:, g_first:g_end].rearrange("p g x -> p (g x)").bitcast(FP8X4),
+                scales=win_scales[:, g_first:g_end].rearrange("p g x -> p (g x)"),
+                in_=win_grouped[:, g_first:g_end].rearrange("p g x t -> p (g x t)"),
+            )
+
+        blocks = [(n, s) for n in range(PIXEL_TILES) for s in range(HIDDEN_PASSES)]
+
+        hidden_blocks = {}
+
+        def first_layer(i, pair, order):
+            n, s = blocks[i]
+            if pair == 0:
+                hidden_blocks[i] = h_pool.tile([P, PACK, PIXEL_TILE], BF16, name="hidden", bufs=HIDDEN_BUFS)
+            win_codes, win_scales = win_operands[n]
+            banks = {}
+            for j, g in order:
+                q, t = 2 * s + pair, 2 * pair + j
+                if g == 0:
+                    banks[j] = psum.tile([P, PIXEL_TILE], F32, name="hidden_bank", tag="bank")
+                nc.tensor.matmul_mx(
+                    out=banks[j][:],
+                    lhsT=w1_codes[:, q, g, P * j : P * (j + 1)].bitcast(FP8X4),
+                    lhsT_scale=w1_scales[:, q, g, P * j : P * (j + 1)],
+                    rhs=win_codes[:, g, :].bitcast(FP8X4),
+                    rhs_scale=win_scales[:, g, :],
+                    start=(g == 0),
+                    stop=(g == CHANNEL_PASSES - 1),
+                )
+                if g == CHANNEL_PASSES - 1:
+                    nc.scalar.activation(
+                        out=hidden_blocks[i][:, t, :], in_=banks[j][:], func=ACT.Relu, bias=bias1[:, s, t : t + 1]
                     )
-                nc.scalar.activation(out=hidden[:, t, :], in_=bank[:], func=ACT.Relu, bias=bias1[:, s, t : t + 1])
-            return hidden
 
         def regroup_hidden(hidden):
-            h_grouped = h_pool.tile([P, PIXEL_TILE, PACK], BF16, name="h_grouped", align_bytes=64)
+            h_grouped = h_pool.tile([P, PIXEL_TILE, PACK], BF16, name="h_grouped", align_bytes=64, bufs=4)
             regroup(nc, h_grouped[:], hidden[:])
             return h_grouped
 
@@ -264,46 +293,72 @@ def tile_localpredictor_pa_kernel(tc, z, W1, b1, W2, b2, out):
                 nc.scalar.activation(out=result[:], in_=out_banks[n][:], func=ACT.Identity, bias=bias2[:, 0:1])
                 nc.sync.dma_start(out=out_maps[b, :, PIXEL_TILE * half : PIXEL_TILE * (half + 1)], in_=result[:])
 
-        compacted = compact_w1(0)
-        prepare_small_operands()
-        for s in range(W1_AHEAD):
-            w1_grouped_tiles = transpose_w1(compacted)
-            if s + 1 < W1_AHEAD:
-                compacted = compact_w1(s + 1)
-            else:
-                windows = {0: gather_windows(0)}
-            quantise_w1(s, w1_grouped_tiles)
-        win_operands = {0: quantise_windows(windows[0])}
-        prepare_w2()
+        compacting_engine = {q: nc.scalar.copy if q in COMPACTED_BY_SCALAR else nc.vector.tensor_copy for q in range(PAIRS)}
+        windows = {0: start_windows(0)}
+        w1_grouped_tiles = {}
+        halves = {}
 
-        blocks = [(n, s) for n in range(PIXEL_TILES) for s in range(HIDDEN_PASSES)]
-        hidden_blocks = {}
+        def compact(q):
+            if q < PAIRS:
+                halves[q] = compact_w1(q, compacting_engine[q])
+
+        def turn(q):
+            if q < PAIRS:
+                w1_grouped_tiles[q] = transpose_w1(halves[q])
+
+        def quantise(q):
+            if q < PAIRS:
+                quantise_w1(q, w1_grouped_tiles[q])
+
+        for q in range(2):
+            compact(q)
+            turn(q)
+        quantise(0)
+        gather_windows(0, 0, windows[0])
+        quantise(1)
+        gather_windows(0, 1, windows[0])
+        quantise_windows(0, 0, 1, windows[0])
+        quantise_windows(0, 1, 2, windows[0])
+        compact(2)
+        compact(3)
+
+        tile_major = [(j, g) for j in range(2) for g in range(CHANNEL_PASSES)]
+        pass_major = [(j, g) for g in range(CHANNEL_PASSES) for j in range(2)]
         grouped_blocks = {}
         quantised_blocks = {}
-        for i in range(len(blocks) + REGROUP_LAG + 2):
-            in_first_layer = i < len(blocks)
-            prepare_next_w1 = in_first_layer and i + W1_AHEAD < HIDDEN_PASSES
-            if in_first_layer:
+        for h in range(2 * len(blocks) + OUTPUT_LAG):
+            i, pair = divmod(h, 2)
+            in_first = i < len(blocks)
+            if in_first:
+                first_layer(i, pair, pass_major if h == 0 else tile_major)
                 n, s = blocks[i]
-                if prepare_next_w1:
-                    compacted = compact_w1(s + W1_AHEAD)
-                hidden_blocks[i] = first_layer(s, win_operands[n][0], win_operands[n][1])
-                if prepare_next_w1:
-                    w1_grouped_tiles = transpose_w1(compacted)
-            to_regroup = i - REGROUP_LAG
-            if 0 <= to_regroup < len(blocks):
-                grouped_blocks[to_regroup] = regroup_hidden(hidden_blocks[to_regroup])
-            to_quantise = to_regroup - 1
-            if 0 <= to_quantise < len(blocks):
-                quantised_blocks[to_quantise] = quantise_hidden(grouped_blocks[to_quantise])
-            if in_first_layer and n + 1 < PIXEL_TILES:
-                if s == 0:
-                    windows[n + 1] = gather_windows(n + 1)
-                if s == 1:
-                    win_operands[n + 1] = quantise_windows(windows[n + 1])
-            if prepare_next_w1:
-                quantise_w1(s + W1_AHEAD, w1_grouped_tiles)
-            to_multiply = to_quantise - 1
-            if to_multiply >= 0:
-                n2, s2 = blocks[to_multiply]
-                second_layer(n2, s2, quantised_blocks[to_multiply][0], quantised_blocks[to_multiply][1])
+            if h == 0:
+                turn(2)
+            turn(h + 3)
+            compact(h + 4)
+            quantise(h + 2)
+            k = (h - REGROUP_LAG) // 2
+            if 0 <= k < len(blocks):
+                if (h - REGROUP_LAG) % 2 == 0:
+                    grouped_blocks[k] = regroup_hidden(hidden_blocks[k])
+            k2 = (h - REGROUP_LAG - QUANT_LAG) // 2
+            if 0 <= k2 < len(blocks) and (h - REGROUP_LAG - QUANT_LAG) % 2 == 0:
+                    quantised_blocks[k2] = quantise_hidden(grouped_blocks[k2])
+            if in_first and n + 1 < PIXEL_TILES:
+                r = 2 * s + pair
+                f = FIRST_GATHER if n == 0 else GATHER_STEP
+                if r == f:
+                    windows[n + 1] = start_windows(n + 1)
+                    gather_windows(n + 1, 0, windows[n + 1])
+                if r == f + SPREAD:
+                    gather_windows(n + 1, 1, windows[n + 1])
+                if r == f + 2 * SPREAD:
+                    quantise_windows(n + 1, 0, CHANNEL_PASSES, windows[n + 1])
+            if h == W2_STEP:
+                prepare_w2()
+            if h == MAP_STEP:
+                load_second_map()
+            k3 = (h - OUTPUT_LAG) // 2
+            if 0 <= k3 < len(blocks) and (h - OUTPUT_LAG) % 2 == 1:
+                n2, s2 = blocks[k3]
+                second_layer(n2, s2, quantised_blocks[k3][0], quantised_blocks[k3][1])

@@ -39,8 +39,8 @@ COMPACTED_BY_SCALAR = (2,)
 OUTPUT_LAG = 9
 QUANT_LAG = 3
 GATHER_STEP = 1
-FIRST_GATHER = 3
-MAP_STEP = 6
+FIRST_GATHER = 2
+MAP_STEP = 4
 SPREAD = 1
 W2_STEP = 5
 REGROUP_LAG = 3
@@ -102,7 +102,11 @@ def tile_localpredictor_pa_kernel(tc, z, W1, b1, W2, b2, out):
 
         def load_map(b):
             z_rows[b] = keep.tile([P, SIDE, SIDE], BF16, name="z_rows%d" % b)
-            nc.sync.dma_start(out=z_rows[b][:].rearrange("c i j -> c (i j)"), in_=z_maps[b])
+            for g in range(CHANNEL_PASSES):
+                nc.sync.dma_start(
+                    out=z_rows[b][g:P:2].rearrange("c i j -> c (i j)"),
+                    in_=z_maps[b, PASS_CHANNELS * g : PASS_CHANNELS * (g + 1)],
+                )
 
         def pad_map(b):
             for t in range(PACK):
@@ -117,7 +121,7 @@ def tile_localpredictor_pa_kernel(tc, z, W1, b1, W2, b2, out):
             b, half = divmod(n, TILES_PER_MAP)
             shifted[n, g] = shift_pool.tile([P, PACK, TILE_ROWS * PITCH], BF16, name="shifted_maps")
             first = BASE + TILE_ROWS * PITCH * half
-            channels = slice(PASS_CHANNELS * g, PASS_CHANNELS * (g + 1))
+            channels = slice(g, P, 2)
             nc.sync.dma_start(
                 out=shifted[n, g][0:P:2, :, :],
                 in_=padded[b][channels, :, first : first + TILE_ROWS * PITCH],

@@ -29,13 +29,17 @@ PIXEL_TILE = 512
 TILES_PER_MAP = MAP // PIXEL_TILE
 PIXEL_TILES = BATCH * TILES_PER_MAP
 TILE_ROWS = PIXEL_TILE // SIDE
-PITCH = SIDE + 1
-BASE = PITCH + 1
-PADDED = BASE + SIDE * PITCH + BASE
-LOADED_FIRST = 2
+BASE = 2 * SIDE + 32
+WHOLE = 1
+MOVES = (
+    (0, slice(0, 4), slice(0, 4), 0),
+    (1, slice(0, 2), slice(2, 4), -1),
+    (1, slice(2, 3), slice(1, 2), 2),
+    (1, slice(3, 4), slice(2, 3), 1),
+)
+AHEAD = 3
 RUN = 4
 HIDDEN_BUFS = 6
-COMPACTED_BY_SCALAR = (2,)
 OUTPUT_LAG = 9
 QUANT_LAG = 3
 GATHER_STEP = 1
@@ -56,7 +60,7 @@ def window_position(u, t):
 
 def pixel_shift(u, t):
     position = window_position(u, t)
-    return PITCH * (position // 3 - 1) + (position % 3 - 1)
+    return SIDE * (position // 3 - 1) + (position % 3 - 1)
 
 
 def regroup(nc, grouped, planes):
@@ -94,43 +98,48 @@ def tile_localpredictor_pa_kernel(tc, z, W1, b1, W2, b2, out):
             nc.sync.dma_start(out=w1_raw[:], in_=w1_rows[s, :, 2 * pair : 2 * pair + 2, :])
             w1_raw_tiles[q] = w1_raw
 
-        padded = {}
+        moved = {}
         for b in range(BATCH):
-            padded[b] = keep.tile([P, PACK, PADDED], BF16, name="padded%d" % b)
-            nc.gpsimd.memset(padded[b][:].rearrange("c t f -> c (t f)").bitcast(U32), 0)
-        z_rows = {}
+            moved[b] = keep.tile([P, PACK, BASE + MAP + BASE], BF16, name="moved%d" % b)
+
+        def map_of(b, t):
+            first = BASE - pixel_shift(0, t)
+            return moved[b][:, t, first : first + MAP]
+
+        def dropped_column(t):
+            return {0: SIDE - 1, 1: None, 2: 0}[window_position(0, t) % 3]
+
+        for b in range(BATCH):
+            for t in range(PACK):
+                first = BASE - pixel_shift(0, t)
+                for zeros in (slice(0, first), slice(first + MAP, None)) if t == WHOLE else (slice(None),):
+                    nc.gpsimd.memset(moved[b][:, t, zeros].bitcast(U32), 0)
 
         def load_map(b):
-            z_rows[b] = keep.tile([P, SIDE, SIDE], BF16, name="z_rows%d" % b)
             for g in range(CHANNEL_PASSES):
                 nc.sync.dma_start(
-                    out=z_rows[b][g:P:2].rearrange("c i j -> c (i j)"),
+                    out=map_of(b, WHOLE)[g:P:2],
                     in_=z_maps[b, PASS_CHANNELS * g : PASS_CHANNELS * (g + 1)],
                 )
 
-        def pad_map(b):
+        def move_map(b):
+            whole = map_of(b, WHOLE).rearrange("c (i j) -> c i j", j=SIDE)
             for t in range(PACK):
-                first = BASE - pixel_shift(0, t)
-                rows = padded[b][:, t, first : first + SIDE * PITCH].rearrange("c (i j) -> c i j", j=PITCH)
-                copy = nc.scalar.copy if t in (0, 3) else nc.vector.tensor_copy
-                copy(out=rows[:, :, 0:SIDE], in_=z_rows[b][:])
+                if t != WHOLE:
+                    kept = slice(0, SIDE - 1) if dropped_column(t) else slice(1, SIDE)
+                    copy = nc.scalar.copy if t == 3 else nc.vector.tensor_copy
+                    copy(out=map_of(b, t).rearrange("c (i j) -> c i j", j=SIDE)[:, :, kept], in_=whole[:, :, kept])
 
         shifted = {}
 
         def load_shifted(n, g):
             b, half = divmod(n, TILES_PER_MAP)
-            shifted[n, g] = shift_pool.tile([P, PACK, TILE_ROWS * PITCH], BF16, name="shifted_maps")
-            first = BASE + TILE_ROWS * PITCH * half
-            channels = slice(g, P, 2)
-            nc.sync.dma_start(
-                out=shifted[n, g][0:P:2, :, :],
-                in_=padded[b][channels, :, first : first + TILE_ROWS * PITCH],
-            )
-            for values in (slice(0, PACK, 3), slice(1, 3)):
-                step = pixel_shift(1, values.start) - pixel_shift(0, values.start)
+            shifted[n, g] = shift_pool.tile([P, PACK, PIXEL_TILE], BF16, name="shifted_maps")
+            for u, values, source, rows in MOVES:
+                first = BASE + PIXEL_TILE * half + SIDE * rows
                 nc.sync.dma_start(
-                    out=shifted[n, g][1:P:2, values, :],
-                    in_=padded[b][channels, values, first + step : first + step + TILE_ROWS * PITCH],
+                    out=shifted[n, g][u:P:2, values],
+                    in_=moved[b][g:P:2, source, first : first + PIXEL_TILE],
                 )
 
         bias1 = keep.tile([P, HIDDEN_PASSES, PACK], BF16, name="bias1")
@@ -138,12 +147,12 @@ def tile_localpredictor_pa_kernel(tc, z, W1, b1, W2, b2, out):
         bias2 = keep.tile([P, 1], BF16, name="bias2")
         nc.scalar.dma_start(out=bias2[:], in_=b2.rearrange("(k o) -> k o", o=1))
         load_map(0)
-        for q in range(LOADED_FIRST):
+        for q in range(AHEAD):
             load_w1(q)
-        pad_map(0)
+        move_map(0)
         for g in range(CHANNEL_PASSES):
             load_shifted(0, g)
-        for q in range(LOADED_FIRST, PAIRS):
+        for q in range(AHEAD, PAIRS):
             load_w1(q)
         for g in range(CHANNEL_PASSES):
             load_shifted(1, g)
@@ -152,7 +161,7 @@ def tile_localpredictor_pa_kernel(tc, z, W1, b1, W2, b2, out):
         load_map(1)
 
         def load_second_map():
-            pad_map(1)
+            move_map(1)
             for n in range(TILES_PER_MAP, PIXEL_TILES):
                 for g in range(CHANNEL_PASSES):
                     load_shifted(n, g)
@@ -160,11 +169,11 @@ def tile_localpredictor_pa_kernel(tc, z, W1, b1, W2, b2, out):
         w1_codes = keep.tile([P, 2 * HIDDEN_PASSES, CHANNEL_PASSES, 2 * P], U32, name="w1_codes", align_bytes=64)
         w1_scales = keep.tile([P, 2 * HIDDEN_PASSES, CHANNEL_PASSES, 2 * P], U8, name="w1_scales", align_bytes=64)
 
-        def compact_w1(q, copy):
+        def compact_w1(q):
             halves = stage.tile([P, 2, 2, K_PASS], BF16, name="halves")
             by_channel = w1_raw_tiles[q][:].rearrange("m j (c x) -> m j c x", x=WINDOW)
             for a in range(2):
-                copy(
+                nc.vector.tensor_copy(
                     out=halves[:, a].rearrange("m j (c r) -> m j c r", r=PACK),
                     in_=by_channel[:, :, :, 5 * a : 5 * a + PACK],
                 )
@@ -220,11 +229,7 @@ def tile_localpredictor_pa_kernel(tc, z, W1, b1, W2, b2, out):
             return win_grouped
 
         def gather_windows(n, g, win_grouped):
-            rows = shifted[n, g][:].rearrange("p t (r j) -> p t r j", j=PITCH)[:, :, :, 0:SIDE]
-            nc.vector.tensor_copy(
-                out=win_grouped[:, g].rearrange("p (r x i) t -> p r x t i", r=TILE_ROWS, i=RUN),
-                in_=rows.rearrange("p t r (x i) -> p r x t i", i=RUN),
-            )
+            regroup(nc, win_grouped[:, g], shifted[n, g][:])
 
         def quantise_windows(n, g_first, g_end, win_grouped):
             win_codes, win_scales = win_operands[n]
@@ -297,14 +302,13 @@ def tile_localpredictor_pa_kernel(tc, z, W1, b1, W2, b2, out):
                 nc.scalar.activation(out=result[:], in_=out_banks[n][:], func=ACT.Identity, bias=bias2[:, 0:1])
                 nc.sync.dma_start(out=out_maps[b, :, PIXEL_TILE * half : PIXEL_TILE * (half + 1)], in_=result[:])
 
-        compacting_engine = {q: nc.scalar.copy if q in COMPACTED_BY_SCALAR else nc.vector.tensor_copy for q in range(PAIRS)}
         windows = {0: start_windows(0)}
         w1_grouped_tiles = {}
         halves = {}
 
         def compact(q):
             if q < PAIRS:
-                halves[q] = compact_w1(q, compacting_engine[q])
+                halves[q] = compact_w1(q)
 
         def turn(q):
             if q < PAIRS:
@@ -314,17 +318,17 @@ def tile_localpredictor_pa_kernel(tc, z, W1, b1, W2, b2, out):
             if q < PAIRS:
                 quantise_w1(q, w1_grouped_tiles[q])
 
-        for q in range(2):
+        for q in range(AHEAD):
             compact(q)
             turn(q)
-        quantise(0)
+            if q > 0:
+                quantise(q - 1)
         gather_windows(0, 0, windows[0])
-        quantise(1)
         gather_windows(0, 1, windows[0])
         quantise_windows(0, 0, 1, windows[0])
         quantise_windows(0, 1, 2, windows[0])
-        compact(2)
-        compact(3)
+        quantise(AHEAD - 1)
+        compact(AHEAD)
 
         tile_major = [(j, g) for j in range(2) for g in range(CHANNEL_PASSES)]
         pass_major = [(j, g) for g in range(CHANNEL_PASSES) for j in range(2)]
@@ -336,11 +340,10 @@ def tile_localpredictor_pa_kernel(tc, z, W1, b1, W2, b2, out):
             if in_first:
                 first_layer(i, pair, pass_major if h == 0 else tile_major)
                 n, s = blocks[i]
-            if h == 0:
-                turn(2)
-            turn(h + 3)
-            compact(h + 4)
-            quantise(h + 2)
+            turn(h + AHEAD)
+            compact(h + AHEAD + 1)
+            if h > 0:
+                quantise(h + AHEAD - 1)
             k = (h - REGROUP_LAG) // 2
             if 0 <= k < len(blocks):
                 if (h - REGROUP_LAG) % 2 == 0:

@@ -30,13 +30,13 @@ TILES_PER_MAP = MAP // PIXEL_TILE
 PIXEL_TILES = BATCH * TILES_PER_MAP
 TILE_ROWS = PIXEL_TILE // SIDE
 BASE = 2 * SIDE + 32
-WHOLE = 1
 MOVES = (
     (0, slice(0, 4), slice(0, 4), 0),
     (1, slice(0, 2), slice(2, 4), -1),
     (1, slice(2, 3), slice(1, 2), 2),
     (1, slice(3, 4), slice(2, 3), 1),
 )
+TAIL_PIECES = 2
 AHEAD = 3
 RUN = 4
 HIDDEN_BUFS = 6
@@ -84,8 +84,8 @@ def tile_localpredictor_pa_kernel(tc, z, W1, b1, W2, b2, out):
         shift_pool = ctx.enter_context(tc.tile_pool(name="shift_pool", bufs=2 * CHANNEL_PASSES))
         win_pool = ctx.enter_context(tc.tile_pool(name="win_pool", bufs=2))
         h_pool = ctx.enter_context(tc.tile_pool(name="h_pool", bufs=5))
-        psum = ctx.enter_context(tc.psum_pool(name="psum", bufs=7))
-        psum_out = ctx.enter_context(tc.psum_pool(name="psum_out", bufs=1))
+        psum = ctx.enter_context(tc.psum_pool(name="psum", bufs=6))
+        psum_out = ctx.enter_context(tc.psum_pool(name="psum_out", bufs=2))
 
         identity = keep.tile([P, P], F32, name="identity")
         make_identity(nc, identity[:])
@@ -98,37 +98,38 @@ def tile_localpredictor_pa_kernel(tc, z, W1, b1, W2, b2, out):
             nc.sync.dma_start(out=w1_raw[:], in_=w1_rows[s, :, 2 * pair : 2 * pair + 2, :])
             w1_raw_tiles[q] = w1_raw
 
+        def dropped_column(t):
+            return (SIDE - 1, None, 0)[window_position(0, t) % 3]
+
         moved = {}
         for b in range(BATCH):
             moved[b] = keep.tile([P, PACK, BASE + MAP + BASE], BF16, name="moved%d" % b)
 
-        def map_of(b, t):
-            first = BASE - pixel_shift(0, t)
-            return moved[b][:, t, first : first + MAP]
-
-        def dropped_column(t):
-            return {0: SIDE - 1, 1: None, 2: 0}[window_position(0, t) % 3]
-
-        for b in range(BATCH):
+            nc.vector.memset(moved[b][:, :, 0 : BASE + 2 * SIDE], 0.0)
+            nc.vector.memset(moved[b][:, :, BASE + MAP - 2 * SIDE :], 0.0)
             for t in range(PACK):
-                first = BASE - pixel_shift(0, t)
-                for zeros in (slice(0, first), slice(first + MAP, None)) if t == WHOLE else (slice(None),):
-                    nc.gpsimd.memset(moved[b][:, t, zeros].bitcast(U32), 0)
+                if dropped_column(t) is not None:
+                    first = BASE - pixel_shift(0, t)
+                    nc.vector.memset(moved[b][:, t, first + dropped_column(t) : first + MAP : SIDE], 0.0)
+        z_rows = {}
 
         def load_map(b):
+            z_rows[b] = keep.tile([P, SIDE, SIDE], BF16, name="z_rows%d" % b)
             for g in range(CHANNEL_PASSES):
                 nc.sync.dma_start(
-                    out=map_of(b, WHOLE)[g:P:2],
+                    out=z_rows[b][g:P:2].rearrange("c i j -> c (i j)"),
                     in_=z_maps[b, PASS_CHANNELS * g : PASS_CHANNELS * (g + 1)],
                 )
 
         def move_map(b):
-            whole = map_of(b, WHOLE).rearrange("c (i j) -> c i j", j=SIDE)
             for t in range(PACK):
-                if t != WHOLE:
-                    kept = slice(0, SIDE - 1) if dropped_column(t) else slice(1, SIDE)
-                    copy = nc.scalar.copy if t == 3 else nc.vector.tensor_copy
-                    copy(out=map_of(b, t).rearrange("c (i j) -> c i j", j=SIDE)[:, :, kept], in_=whole[:, :, kept])
+                first = BASE - pixel_shift(0, t)
+                rows = moved[b][:, t, first : first + MAP].rearrange("c (i j) -> c i j", j=SIDE)
+                if dropped_column(t) is None:
+                    nc.scalar.copy(out=rows, in_=z_rows[b][:])
+                else:
+                    kept = slice(1, SIDE) if dropped_column(t) == 0 else slice(0, SIDE - 1)
+                    nc.vector.tensor_copy(out=rows[:, :, kept], in_=z_rows[b][:, :, kept])
 
         shifted = {}
 
@@ -267,40 +268,54 @@ def tile_localpredictor_pa_kernel(tc, z, W1, b1, W2, b2, out):
                         out=hidden_blocks[i][:, t, :], in_=banks[j][:], func=ACT.Relu, bias=bias1[:, s, t : t + 1]
                     )
 
-        def regroup_hidden(hidden):
-            h_grouped = h_pool.tile([P, PIXEL_TILE, PACK], BF16, name="h_grouped", align_bytes=64, bufs=4)
-            regroup(nc, h_grouped[:], hidden[:])
-            return h_grouped
+        def pieces(count):
+            width = PIXEL_TILE // count
+            return [slice(width * piece, width * (piece + 1)) for piece in range(count)]
 
-        def quantise_hidden(h_grouped):
-            h_codes = h_pool.tile([P, PIXEL_TILE], U32, name="h_codes", align_bytes=64)
-            h_scales = h_pool.tile([P, PIXEL_TILE], U8, name="h_scales", align_bytes=64)
+        grouped_blocks = {}
+        quantised_blocks = {}
+
+        def regroup_hidden(i, columns):
+            if columns.start == 0:
+                grouped_blocks[i] = h_pool.tile([P, PIXEL_TILE, PACK], BF16, name="h_grouped", align_bytes=64, bufs=4)
+            regroup(nc, grouped_blocks[i][:, columns], hidden_blocks[i][:, :, columns])
+
+        def quantise_hidden(i, columns):
+            if columns.start == 0:
+                h_codes = h_pool.tile([P, PIXEL_TILE], U32, name="h_codes", align_bytes=64)
+                h_scales = h_pool.tile([P, PIXEL_TILE], U8, name="h_scales", align_bytes=64)
+                quantised_blocks[i] = (h_codes, h_scales)
+            codes, scales = quantised_blocks[i]
             nc.vector.quantize_mx(
-                out=h_codes[:].bitcast(FP8X4),
-                scales=h_scales[:],
-                in_=h_grouped[:].rearrange("p x t -> p (x t)"),
+                out=codes[:, columns].bitcast(FP8X4),
+                scales=scales[:, columns],
+                in_=grouped_blocks[i][:, columns].rearrange("p x t -> p (x t)"),
             )
-            return h_codes, h_scales
 
         out_banks = {}
 
-        def second_layer(n, s, h_codes, h_scales):
+        def second_layer(i, columns):
+            n, s = blocks[i]
+            codes, scales = quantised_blocks[i]
+            width = columns.stop - columns.start
             if s == 0:
-                out_banks[n] = psum_out.tile([P, PIXEL_TILE], F32, name="out_bank")
+                out_banks[n, columns.start] = psum_out.tile([P, width], F32, name="out_bank")
+            out_bank = out_banks[n, columns.start]
             nc.tensor.matmul_mx(
-                out=out_banks[n][:],
+                out=out_bank[:],
                 lhsT=w2_codes[:, s, :].bitcast(FP8X4),
                 lhsT_scale=w2_scales[:, s, :],
-                rhs=h_codes[:].bitcast(FP8X4),
-                rhs_scale=h_scales[:],
+                rhs=codes[:, columns].bitcast(FP8X4),
+                rhs_scale=scales[:, columns],
                 start=(s == 0),
                 stop=(s == HIDDEN_PASSES - 1),
             )
             if s == HIDDEN_PASSES - 1:
                 b, half = divmod(n, TILES_PER_MAP)
-                result = stage.tile([P, PIXEL_TILE], F32, name="result")
-                nc.scalar.activation(out=result[:], in_=out_banks[n][:], func=ACT.Identity, bias=bias2[:, 0:1])
-                nc.sync.dma_start(out=out_maps[b, :, PIXEL_TILE * half : PIXEL_TILE * (half + 1)], in_=result[:])
+                result = stage.tile([P, width], F32, name="result")
+                nc.scalar.activation(out=result[:], in_=out_bank[:], func=ACT.Identity, bias=bias2[:, 0:1])
+                first = PIXEL_TILE * half + columns.start
+                nc.sync.dma_start(out=out_maps[b, :, first : first + width], in_=result[:])
 
         windows = {0: start_windows(0)}
         w1_grouped_tiles = {}
@@ -323,17 +338,14 @@ def tile_localpredictor_pa_kernel(tc, z, W1, b1, W2, b2, out):
             turn(q)
             if q > 0:
                 quantise(q - 1)
-        gather_windows(0, 0, windows[0])
-        gather_windows(0, 1, windows[0])
-        quantise_windows(0, 0, 1, windows[0])
-        quantise_windows(0, 1, 2, windows[0])
+        for g in range(CHANNEL_PASSES):
+            gather_windows(0, g, windows[0])
+            quantise_windows(0, g, g + 1, windows[0])
         quantise(AHEAD - 1)
         compact(AHEAD)
 
         tile_major = [(j, g) for j in range(2) for g in range(CHANNEL_PASSES)]
         pass_major = [(j, g) for g in range(CHANNEL_PASSES) for j in range(2)]
-        grouped_blocks = {}
-        quantised_blocks = {}
         for h in range(2 * len(blocks) + OUTPUT_LAG):
             i, pair = divmod(h, 2)
             in_first = i < len(blocks)
@@ -347,10 +359,12 @@ def tile_localpredictor_pa_kernel(tc, z, W1, b1, W2, b2, out):
             k = (h - REGROUP_LAG) // 2
             if 0 <= k < len(blocks):
                 if (h - REGROUP_LAG) % 2 == 0:
-                    grouped_blocks[k] = regroup_hidden(hidden_blocks[k])
+                    for columns in pieces(TAIL_PIECES if k == len(blocks) - 1 else 1):
+                        regroup_hidden(k, columns)
             k2 = (h - REGROUP_LAG - QUANT_LAG) // 2
             if 0 <= k2 < len(blocks) and (h - REGROUP_LAG - QUANT_LAG) % 2 == 0:
-                    quantised_blocks[k2] = quantise_hidden(grouped_blocks[k2])
+                    for columns in pieces(TAIL_PIECES if k2 == len(blocks) - 1 else 1):
+                        quantise_hidden(k2, columns)
             if in_first and n + 1 < PIXEL_TILES:
                 r = 2 * s + pair
                 f = FIRST_GATHER if n == 0 else GATHER_STEP
@@ -367,5 +381,5 @@ def tile_localpredictor_pa_kernel(tc, z, W1, b1, W2, b2, out):
                 load_second_map()
             k3 = (h - OUTPUT_LAG) // 2
             if 0 <= k3 < len(blocks) and (h - OUTPUT_LAG) % 2 == 1:
-                n2, s2 = blocks[k3]
-                second_layer(n2, s2, quantised_blocks[k3][0], quantised_blocks[k3][1])
+                for columns in pieces(TAIL_PIECES if blocks[k3][0] == PIXEL_TILES - 1 else 1):
+                    second_layer(k3, columns)

@@ -37,6 +37,7 @@ MOVES = (
     (1, slice(3, 4), slice(2, 3), 1),
 )
 TAIL_PIECES = 2
+RUN_PAIRS = 2
 AHEAD = 3
 RUN = 4
 HIDDEN_BUFS = 6
@@ -342,7 +343,8 @@ def tile_localpredictor_pa_kernel(tc, z, W1, b1, W2, b2, out):
             gather_windows(0, g, windows[0])
             quantise_windows(0, g, g + 1, windows[0])
         quantise(AHEAD - 1)
-        compact(AHEAD)
+        for q in range(AHEAD, AHEAD + RUN_PAIRS):
+            compact(q)
 
         tile_major = [(j, g) for j in range(2) for g in range(CHANNEL_PASSES)]
         pass_major = [(j, g) for g in range(CHANNEL_PASSES) for j in range(2)]
@@ -352,8 +354,11 @@ def tile_localpredictor_pa_kernel(tc, z, W1, b1, W2, b2, out):
             if in_first:
                 first_layer(i, pair, pass_major if h == 0 else tile_major)
                 n, s = blocks[i]
-            turn(h + AHEAD)
-            compact(h + AHEAD + 1)
+            if h % RUN_PAIRS == 0:
+                for q in range(h + AHEAD, h + AHEAD + RUN_PAIRS):
+                    turn(q)
+                for q in range(h + AHEAD + RUN_PAIRS, h + AHEAD + 2 * RUN_PAIRS):
+                    compact(q)
             if h > 0:
                 quantise(h + AHEAD - 1)
             k = (h - REGROUP_LAG) // 2

@@ -36,6 +36,7 @@ MOVES = (
     (1, slice(2, 3), slice(1, 2), 2),
     (1, slice(3, 4), slice(2, 3), 1),
 )
+FLUSHED = 4
 TAIL_PIECES = 2
 RUN_PAIRS = 2
 AHEAD = 3
@@ -202,15 +203,22 @@ def tile_localpredictor_pa_kernel(tc, z, W1, b1, W2, b2, out):
         w2_codes = keep.tile([P, HIDDEN_PASSES, P], U32, name="w2_codes", align_bytes=64)
         w2_scales = keep.tile([P, HIDDEN_PASSES, P], U8, name="w2_scales", align_bytes=64)
 
+        w2_words = keep.tile([P, HIDDEN_PASSES, 2, P], F32, name="w2_words")
+
+        def part_w2():
+            nc.vector.tensor_copy(
+                out=w2_words[:], in_=w2_rows[:].bitcast(F32).rearrange("k (h p u) -> k h u p", h=HIDDEN_PASSES, u=2)
+            )
+
         def prepare_w2():
-            words = w2_rows[:].bitcast(F32)
+            words = w2_words[:]
             w2_grouped = keep.tile([P, HIDDEN_PASSES * P, 2], F32, name="w2_grouped", align_bytes=64)
             for pair in range(HIDDEN_PASSES // 2):
                 bank = psum.tile([P, 2, 2, P], F32, tag="bank")
                 for u in range(2):
                     for j in range(2):
                         s = 2 * pair + j
-                        nc.tensor.transpose(bank[:, u, j, :], words[:, 2 * P * s + u : 2 * P * (s + 1) : 2], identity[:])
+                        nc.tensor.transpose(bank[:, u, j, :], words[:, s, u, :], identity[:])
                 nc.scalar.copy(
                     out=w2_grouped[:, 2 * P * pair : 2 * P * (pair + 1), :],
                     in_=bank[:].rearrange("p u j k -> p (j k) u"),
@@ -241,26 +249,33 @@ def tile_localpredictor_pa_kernel(tc, z, W1, b1, W2, b2, out):
                 in_=win_grouped[:, g_first:g_end].rearrange("p g x t -> p (g x t)"),
             )
 
-        blocks = [(n, s) for n in range(PIXEL_TILES) for s in range(HIDDEN_PASSES)]
+        def pieces(count):
+            width = PIXEL_TILE // count
+            return [slice(width * piece, width * (piece + 1)) for piece in range(count)]
+
+        blocks = [(n, s, columns) for n in range(PIXEL_TILES) for s in range(HIDDEN_PASSES) for columns in pieces(1)]
+        last_tile, last_pass, whole = blocks.pop()
+        blocks.extend((last_tile, last_pass, columns) for columns in pieces(TAIL_PIECES))
 
         hidden_blocks = {}
 
         def first_layer(i, pair, order):
-            n, s = blocks[i]
+            n, s, columns = blocks[i]
+            width = columns.stop - columns.start
             if pair == 0:
-                hidden_blocks[i] = h_pool.tile([P, PACK, PIXEL_TILE], BF16, name="hidden", bufs=HIDDEN_BUFS)
+                hidden_blocks[i] = h_pool.tile([P, PACK, width], BF16, name="hidden", bufs=HIDDEN_BUFS)
             win_codes, win_scales = win_operands[n]
             banks = {}
             for j, g in order:
                 q, t = 2 * s + pair, 2 * pair + j
                 if g == 0:
-                    banks[j] = psum.tile([P, PIXEL_TILE], F32, name="hidden_bank", tag="bank")
+                    banks[j] = psum.tile([P, width], F32, name="hidden_bank", tag="bank")
                 nc.tensor.matmul_mx(
                     out=banks[j][:],
                     lhsT=w1_codes[:, q, g, P * j : P * (j + 1)].bitcast(FP8X4),
                     lhsT_scale=w1_scales[:, q, g, P * j : P * (j + 1)],
-                    rhs=win_codes[:, g, :].bitcast(FP8X4),
-                    rhs_scale=win_scales[:, g, :],
+                    rhs=win_codes[:, g, columns].bitcast(FP8X4),
+                    rhs_scale=win_scales[:, g, columns],
                     start=(g == 0),
                     stop=(g == CHANNEL_PASSES - 1),
                 )
@@ -269,54 +284,53 @@ def tile_localpredictor_pa_kernel(tc, z, W1, b1, W2, b2, out):
                         out=hidden_blocks[i][:, t, :], in_=banks[j][:], func=ACT.Relu, bias=bias1[:, s, t : t + 1]
                     )
 
-        def pieces(count):
-            width = PIXEL_TILE // count
-            return [slice(width * piece, width * (piece + 1)) for piece in range(count)]
-
         grouped_blocks = {}
         quantised_blocks = {}
 
-        def regroup_hidden(i, columns):
-            if columns.start == 0:
-                grouped_blocks[i] = h_pool.tile([P, PIXEL_TILE, PACK], BF16, name="h_grouped", align_bytes=64, bufs=4)
-            regroup(nc, grouped_blocks[i][:, columns], hidden_blocks[i][:, :, columns])
+        def regroup_hidden(i):
+            width = hidden_blocks[i].shape[2]
+            grouped_blocks[i] = h_pool.tile([P, width, PACK], BF16, name="h_grouped", align_bytes=64, bufs=4)
+            regroup(nc, grouped_blocks[i][:], hidden_blocks[i][:])
 
-        def quantise_hidden(i, columns):
-            if columns.start == 0:
-                h_codes = h_pool.tile([P, PIXEL_TILE], U32, name="h_codes", align_bytes=64)
-                h_scales = h_pool.tile([P, PIXEL_TILE], U8, name="h_scales", align_bytes=64)
-                quantised_blocks[i] = (h_codes, h_scales)
-            codes, scales = quantised_blocks[i]
+        def quantise_hidden(i):
+            width = hidden_blocks[i].shape[2]
+            h_codes = h_pool.tile([P, width], U32, name="h_codes", align_bytes=64)
+            h_scales = h_pool.tile([P, width], U8, name="h_scales", align_bytes=64)
             nc.vector.quantize_mx(
-                out=codes[:, columns].bitcast(FP8X4),
-                scales=scales[:, columns],
-                in_=grouped_blocks[i][:, columns].rearrange("p x t -> p (x t)"),
+                out=h_codes[:].bitcast(FP8X4),
+                scales=h_scales[:],
+                in_=grouped_blocks[i][:].rearrange("p x t -> p (x t)"),
             )
+            quantised_blocks[i] = (h_codes, h_scales)
 
         out_banks = {}
 
-        def second_layer(i, columns):
-            n, s = blocks[i]
+        def second_layer(i):
+            n, s, columns = blocks[i]
             codes, scales = quantised_blocks[i]
-            width = columns.stop - columns.start
-            if s == 0:
-                out_banks[n, columns.start] = psum_out.tile([P, width], F32, name="out_bank")
-            out_bank = out_banks[n, columns.start]
-            nc.tensor.matmul_mx(
-                out=out_bank[:],
-                lhsT=w2_codes[:, s, :].bitcast(FP8X4),
-                lhsT_scale=w2_scales[:, s, :],
-                rhs=codes[:, columns].bitcast(FP8X4),
-                rhs_scale=scales[:, columns],
-                start=(s == 0),
-                stop=(s == HIDDEN_PASSES - 1),
-            )
-            if s == HIDDEN_PASSES - 1:
-                b, half = divmod(n, TILES_PER_MAP)
-                result = stage.tile([P, width], F32, name="result")
-                nc.scalar.activation(out=result[:], in_=out_bank[:], func=ACT.Identity, bias=bias2[:, 0:1])
-                first = PIXEL_TILE * half + columns.start
-                nc.sync.dma_start(out=out_maps[b, :, first : first + width], in_=result[:])
+            for piece in pieces(TAIL_PIECES if n == last_tile else 1):
+                if not columns.start <= piece.start < columns.stop:
+                    continue
+                width = piece.stop - piece.start
+                own = slice(piece.start - columns.start, piece.stop - columns.start)
+                if s == 0:
+                    out_banks[n, piece.start] = psum_out.tile([P, width], F32, name="out_bank")
+                out_bank = out_banks[n, piece.start]
+                nc.tensor.matmul_mx(
+                    out=out_bank[:],
+                    lhsT=w2_codes[:, s, :].bitcast(FP8X4),
+                    lhsT_scale=w2_scales[:, s, :],
+                    rhs=codes[:, own].bitcast(FP8X4),
+                    rhs_scale=scales[:, own],
+                    start=(s == 0),
+                    stop=(s == HIDDEN_PASSES - 1),
+                )
+                if s == HIDDEN_PASSES - 1:
+                    b, half = divmod(n, TILES_PER_MAP)
+                    result = stage.tile([P, width], F32, name="result")
+                    nc.scalar.activation(out=result[:], in_=out_bank[:], func=ACT.Identity, bias=bias2[:, 0:1])
+                    first = PIXEL_TILE * half + piece.start
+                    nc.sync.dma_start(out=out_maps[b, :, first : first + width], in_=result[:])
 
         windows = {0: start_windows(0)}
         w1_grouped_tiles = {}
@@ -353,7 +367,7 @@ def tile_localpredictor_pa_kernel(tc, z, W1, b1, W2, b2, out):
             in_first = i < len(blocks)
             if in_first:
                 first_layer(i, pair, pass_major if h == 0 else tile_major)
-                n, s = blocks[i]
+                n, s, columns = blocks[i]
             if h % RUN_PAIRS == 0:
                 for q in range(h + AHEAD, h + AHEAD + RUN_PAIRS):
                     turn(q)
@@ -361,15 +375,12 @@ def tile_localpredictor_pa_kernel(tc, z, W1, b1, W2, b2, out):
                     compact(q)
             if h > 0:
                 quantise(h + AHEAD - 1)
-            k = (h - REGROUP_LAG) // 2
-            if 0 <= k < len(blocks):
-                if (h - REGROUP_LAG) % 2 == 0:
-                    for columns in pieces(TAIL_PIECES if k == len(blocks) - 1 else 1):
-                        regroup_hidden(k, columns)
-            k2 = (h - REGROUP_LAG - QUANT_LAG) // 2
-            if 0 <= k2 < len(blocks) and (h - REGROUP_LAG - QUANT_LAG) % 2 == 0:
-                    for columns in pieces(TAIL_PIECES if k2 == len(blocks) - 1 else 1):
-                        quantise_hidden(k2, columns)
+            for k in range(len(blocks)):
+                quantise_step = 2 * k + REGROUP_LAG + (1 if k >= len(blocks) - FLUSHED else QUANT_LAG)
+                if h == 2 * k + REGROUP_LAG:
+                    regroup_hidden(k)
+                if h == quantise_step:
+                    quantise_hidden(k)
             if in_first and n + 1 < PIXEL_TILES:
                 r = 2 * s + pair
                 f = FIRST_GATHER if n == 0 else GATHER_STEP
@@ -380,11 +391,12 @@ def tile_localpredictor_pa_kernel(tc, z, W1, b1, W2, b2, out):
                     gather_windows(n + 1, 1, windows[n + 1])
                 if r == f + 2 * SPREAD:
                     quantise_windows(n + 1, 0, CHANNEL_PASSES, windows[n + 1])
+            if h == W2_STEP - 1:
+                part_w2()
             if h == W2_STEP:
                 prepare_w2()
             if h == MAP_STEP:
                 load_second_map()
-            k3 = (h - OUTPUT_LAG) // 2
-            if 0 <= k3 < len(blocks) and (h - OUTPUT_LAG) % 2 == 1:
-                for columns in pieces(TAIL_PIECES if blocks[k3][0] == PIXEL_TILES - 1 else 1):
-                    second_layer(k3, columns)
+            k = (h - OUTPUT_LAG) // 2
+            if 0 <= k < len(blocks) and (h - OUTPUT_LAG) % 2 == 1:
+                second_layer(k)

@@ -36,7 +36,7 @@ MOVES = (
     (1, slice(2, 3), slice(1, 2), 2),
     (1, slice(3, 4), slice(2, 3), 1),
 )
-FLUSHED = 4
+FLUSHED = 0
 TAIL_PIECES = 2
 RUN_PAIRS = 2
 AHEAD = 3
@@ -49,7 +49,7 @@ FIRST_GATHER = 2
 MAP_STEP = 4
 SPREAD = 1
 W2_STEP = 5
-REGROUP_LAG = 3
+REGROUP_LAG = 2
 PAIRS = 2 * HIDDEN_PASSES
 PAIRS_AHEAD = 4
 
@@ -65,8 +65,8 @@ def pixel_shift(u, t):
     return SIDE * (position // 3 - 1) + (position % 3 - 1)
 
 
-def regroup(nc, grouped, planes):
-    nc.vector.tensor_copy(
+def regroup(grouped, planes, copy):
+    copy(
         out=grouped.rearrange("p (x i) t -> p x t i", i=RUN),
         in_=planes.rearrange("p t (x i) -> p x t i", i=RUN),
     )
@@ -203,22 +203,15 @@ def tile_localpredictor_pa_kernel(tc, z, W1, b1, W2, b2, out):
         w2_codes = keep.tile([P, HIDDEN_PASSES, P], U32, name="w2_codes", align_bytes=64)
         w2_scales = keep.tile([P, HIDDEN_PASSES, P], U8, name="w2_scales", align_bytes=64)
 
-        w2_words = keep.tile([P, HIDDEN_PASSES, 2, P], F32, name="w2_words")
-
-        def part_w2():
-            nc.vector.tensor_copy(
-                out=w2_words[:], in_=w2_rows[:].bitcast(F32).rearrange("k (h p u) -> k h u p", h=HIDDEN_PASSES, u=2)
-            )
-
         def prepare_w2():
-            words = w2_words[:]
+            words = w2_rows[:].bitcast(F32)
             w2_grouped = keep.tile([P, HIDDEN_PASSES * P, 2], F32, name="w2_grouped", align_bytes=64)
             for pair in range(HIDDEN_PASSES // 2):
                 bank = psum.tile([P, 2, 2, P], F32, tag="bank")
                 for u in range(2):
                     for j in range(2):
                         s = 2 * pair + j
-                        nc.tensor.transpose(bank[:, u, j, :], words[:, s, u, :], identity[:])
+                        nc.tensor.transpose(bank[:, u, j, :], words[:, 2 * P * s + u : 2 * P * (s + 1) : 2], identity[:])
                 nc.scalar.copy(
                     out=w2_grouped[:, 2 * P * pair : 2 * P * (pair + 1), :],
                     in_=bank[:].rearrange("p u j k -> p (j k) u"),
@@ -239,7 +232,7 @@ def tile_localpredictor_pa_kernel(tc, z, W1, b1, W2, b2, out):
             return win_grouped
 
         def gather_windows(n, g, win_grouped):
-            regroup(nc, win_grouped[:, g], shifted[n, g][:])
+            regroup(win_grouped[:, g], shifted[n, g][:], nc.scalar.copy if (n, g) == (0, 1) else nc.vector.tensor_copy)
 
         def quantise_windows(n, g_first, g_end, win_grouped):
             win_codes, win_scales = win_operands[n]
@@ -290,7 +283,7 @@ def tile_localpredictor_pa_kernel(tc, z, W1, b1, W2, b2, out):
         def regroup_hidden(i):
             width = hidden_blocks[i].shape[2]
             grouped_blocks[i] = h_pool.tile([P, width, PACK], BF16, name="h_grouped", align_bytes=64, bufs=4)
-            regroup(nc, grouped_blocks[i][:], hidden_blocks[i][:])
+            regroup(grouped_blocks[i][:], hidden_blocks[i][:], nc.vector.tensor_copy)
 
         def quantise_hidden(i):
             width = hidden_blocks[i].shape[2]
@@ -348,15 +341,19 @@ def tile_localpredictor_pa_kernel(tc, z, W1, b1, W2, b2, out):
             if q < PAIRS:
                 quantise_w1(q, w1_grouped_tiles[q])
 
-        for q in range(AHEAD):
-            compact(q)
-            turn(q)
-            if q > 0:
-                quantise(q - 1)
-        for g in range(CHANNEL_PASSES):
-            gather_windows(0, g, windows[0])
-            quantise_windows(0, g, g + 1, windows[0])
-        quantise(AHEAD - 1)
+        compact(0)
+        turn(0)
+        compact(1)
+        turn(1)
+        quantise(0)
+        compact(2)
+        turn(2)
+        gather_windows(0, 1, windows[0])
+        gather_windows(0, 0, windows[0])
+        quantise(1)
+        quantise_windows(0, 0, 1, windows[0])
+        quantise(2)
+        quantise_windows(0, 1, 2, windows[0])
         for q in range(AHEAD, AHEAD + RUN_PAIRS):
             compact(q)
 
@@ -391,8 +388,6 @@ def tile_localpredictor_pa_kernel(tc, z, W1, b1, W2, b2, out):
                     gather_windows(n + 1, 1, windows[n + 1])
                 if r == f + 2 * SPREAD:
                     quantise_windows(n + 1, 0, CHANNEL_PASSES, windows[n + 1])
-            if h == W2_STEP - 1:
-                part_w2()
             if h == W2_STEP:
                 prepare_w2()
             if h == MAP_STEP:

@@ -38,6 +38,7 @@ MOVES = (
 )
 FLUSHED = 0
 TAIL_PIECES = 2
+PART_LAG = 2
 RUN_PAIRS = 2
 AHEAD = 3
 RUN = 4
@@ -48,7 +49,7 @@ GATHER_STEP = 1
 FIRST_GATHER = 2
 MAP_STEP = 4
 SPREAD = 1
-W2_STEP = 5
+W2_STEP = 6
 REGROUP_LAG = 2
 PAIRS = 2 * HIDDEN_PASSES
 PAIRS_AHEAD = 4
@@ -91,6 +92,8 @@ def tile_localpredictor_pa_kernel(tc, z, W1, b1, W2, b2, out):
 
         identity = keep.tile([P, P], F32, name="identity")
         make_identity(nc, identity[:])
+        table_loaded = keep.tile([P, 1], F32, name="table_loaded")
+        nc.scalar.activation(out=table_loaded[:], in_=identity[:, 0:1], func=ACT.Relu)
 
         w1_raw_tiles = {}
 
@@ -203,15 +206,22 @@ def tile_localpredictor_pa_kernel(tc, z, W1, b1, W2, b2, out):
         w2_codes = keep.tile([P, HIDDEN_PASSES, P], U32, name="w2_codes", align_bytes=64)
         w2_scales = keep.tile([P, HIDDEN_PASSES, P], U8, name="w2_scales", align_bytes=64)
 
+        w2_words = keep.tile([P, HIDDEN_PASSES, 2, P], F32, name="w2_words")
+
+        def part_w2():
+            nc.vector.tensor_copy(
+                out=w2_words[:], in_=w2_rows[:].bitcast(F32).rearrange("k (h p u) -> k h u p", h=HIDDEN_PASSES, u=2)
+            )
+
         def prepare_w2():
-            words = w2_rows[:].bitcast(F32)
+            words = w2_words[:]
             w2_grouped = keep.tile([P, HIDDEN_PASSES * P, 2], F32, name="w2_grouped", align_bytes=64)
             for pair in range(HIDDEN_PASSES // 2):
                 bank = psum.tile([P, 2, 2, P], F32, tag="bank")
                 for u in range(2):
                     for j in range(2):
                         s = 2 * pair + j
-                        nc.tensor.transpose(bank[:, u, j, :], words[:, 2 * P * s + u : 2 * P * (s + 1) : 2], identity[:])
+                        nc.tensor.transpose(bank[:, u, j, :], words[:, s, u, :], identity[:])
                 nc.scalar.copy(
                     out=w2_grouped[:, 2 * P * pair : 2 * P * (pair + 1), :],
                     in_=bank[:].rearrange("p u j k -> p (j k) u"),
@@ -388,6 +398,8 @@ def tile_localpredictor_pa_kernel(tc, z, W1, b1, W2, b2, out):
                     gather_windows(n + 1, 1, windows[n + 1])
                 if r == f + 2 * SPREAD:
                     quantise_windows(n + 1, 0, CHANNEL_PASSES, windows[n + 1])
+            if h == W2_STEP - PART_LAG:
+                part_w2()
             if h == W2_STEP:
                 prepare_w2()
             if h == MAP_STEP:

@@ -29,6 +29,7 @@ PIXEL_TILE = 512
 TILES_PER_MAP = MAP // PIXEL_TILE
 PIXEL_TILES = BATCH * TILES_PER_MAP
 TILE_ROWS = PIXEL_TILE // SIDE
+WHOLE = 1
 BASE = 2 * SIDE + 32
 MOVES = (
     (0, slice(0, 4), slice(0, 4), 0),
@@ -41,7 +42,7 @@ TAIL_PIECES = 2
 PART_LAG = 2
 RUN_PAIRS = 2
 AHEAD = 3
-RUN = 4
+RUN = 8
 HIDDEN_BUFS = 6
 OUTPUT_LAG = 9
 QUANT_LAG = 3
@@ -107,7 +108,8 @@ def tile_localpredictor_pa_kernel(tc, z, W1, b1, W2, b2, out):
             return (SIDE - 1, None, 0)[window_position(0, t) % 3]
 
         moved = {}
-        for b in range(BATCH):
+
+        def clear_gaps(b):
             moved[b] = keep.tile([P, PACK, BASE + MAP + BASE], BF16, name="moved%d" % b)
 
             nc.vector.memset(moved[b][:, :, 0 : BASE + 2 * SIDE], 0.0)
@@ -116,10 +118,20 @@ def tile_localpredictor_pa_kernel(tc, z, W1, b1, W2, b2, out):
                 if dropped_column(t) is not None:
                     first = BASE - pixel_shift(0, t)
                     nc.vector.memset(moved[b][:, t, first + dropped_column(t) : first + MAP : SIDE], 0.0)
+
+        for b in range(BATCH):
+            clear_gaps(b)
         z_rows = {}
 
+        def copy_rows(b, t):
+            first = BASE - pixel_shift(0, t)
+            return moved[b][:, t, first : first + MAP].rearrange("c (i j) -> c i j", j=SIDE)
+
         def load_map(b):
-            z_rows[b] = keep.tile([P, SIDE, SIDE], BF16, name="z_rows%d" % b)
+            if b == 0:
+                z_rows[b] = keep.tile([P, SIDE, SIDE], BF16, name="z_rows")[:]
+            else:
+                z_rows[b] = copy_rows(b, WHOLE)
             for g in range(CHANNEL_PASSES):
                 nc.sync.dma_start(
                     out=z_rows[b][g:P:2].rearrange("c i j -> c (i j)"),
@@ -128,10 +140,10 @@ def tile_localpredictor_pa_kernel(tc, z, W1, b1, W2, b2, out):
 
         def move_map(b):
             for t in range(PACK):
-                first = BASE - pixel_shift(0, t)
-                rows = moved[b][:, t, first : first + MAP].rearrange("c (i j) -> c i j", j=SIDE)
-                if dropped_column(t) is None:
-                    nc.scalar.copy(out=rows, in_=z_rows[b][:])
+                rows = copy_rows(b, t)
+                if t == WHOLE:
+                    if b == 0:
+                        nc.scalar.copy(out=rows, in_=z_rows[b])
                 else:
                     kept = slice(1, SIDE) if dropped_column(t) == 0 else slice(0, SIDE - 1)
                     nc.vector.tensor_copy(out=rows[:, :, kept], in_=z_rows[b][:, :, kept])
@@ -164,7 +176,6 @@ def tile_localpredictor_pa_kernel(tc, z, W1, b1, W2, b2, out):
             load_shifted(1, g)
         w2_rows = keep.tile([P, HIDDEN], BF16, name="w2_rows")
         nc.sync.dma_start(out=w2_rows[:], in_=W2)
-        load_map(1)
 
         def load_second_map():
             move_map(1)
@@ -241,8 +252,8 @@ def tile_localpredictor_pa_kernel(tc, z, W1, b1, W2, b2, out):
             win_operands[n] = (win_codes, win_scales)
             return win_grouped
 
-        def gather_windows(n, g, win_grouped):
-            regroup(win_grouped[:, g], shifted[n, g][:], nc.scalar.copy if (n, g) == (0, 1) else nc.vector.tensor_copy)
+        def gather_windows(n, g, win_grouped, columns=slice(0, PIXEL_TILE), copy=nc.vector.tensor_copy):
+            regroup(win_grouped[:, g, columns], shifted[n, g][:, :, columns], copy)
 
         def quantise_windows(n, g_first, g_end, win_grouped):
             win_codes, win_scales = win_operands[n]
@@ -358,12 +369,15 @@ def tile_localpredictor_pa_kernel(tc, z, W1, b1, W2, b2, out):
         quantise(0)
         compact(2)
         turn(2)
-        gather_windows(0, 1, windows[0])
+        first_half, second_half = pieces(2)
+        gather_windows(0, 1, windows[0], second_half, nc.scalar.copy)
         gather_windows(0, 0, windows[0])
         quantise(1)
+        gather_windows(0, 1, windows[0], first_half)
         quantise_windows(0, 0, 1, windows[0])
         quantise(2)
         quantise_windows(0, 1, 2, windows[0])
+        load_map(1)
         for q in range(AHEAD, AHEAD + RUN_PAIRS):
             compact(q)
 

from contextlib import ExitStack

import concourse.mybir as mybir
from concourse.masks import make_identity

BF16 = mybir.dt.bfloat16
F32 = mybir.dt.float32
U32 = mybir.dt.uint32
U8 = mybir.dt.uint8
FP8X4 = mybir.dt.float8_e4m3fn_x4
ACT = mybir.ActivationFunctionType
ALU = mybir.AluOpType

P = 128
PACK = 4
K_PASS = P * PACK

BATCH = 2
CHANNELS = 128
SIDE = 32
MAP = SIDE * SIDE
WINDOW = 9
HIDDEN = 2048

CHANNEL_PASSES = 2
PASS_CHANNELS = CHANNELS // CHANNEL_PASSES
HIDDEN_PASSES = HIDDEN // K_PASS
PIXEL_TILE = 512
TILES_PER_MAP = MAP // PIXEL_TILE
PIXEL_TILES = BATCH * TILES_PER_MAP
TILE_ROWS = PIXEL_TILE // SIDE
WHOLE = 1
BASE = 2 * SIDE + 32
MOVES = (
    (0, slice(0, 4), slice(0, 4), 0),
    (1, slice(0, 2), slice(2, 4), -1),
    (1, slice(2, 3), slice(1, 2), 2),
    (1, slice(3, 4), slice(2, 3), 1),
)
FLUSHED = 0
TAIL_PIECES = 2
PART_LAG = 2
RUN_PAIRS = 2
AHEAD = 3
RUN = 8
HIDDEN_BUFS = 6
OUTPUT_LAG = 9
QUANT_LAG = 3
GATHER_STEP = 1
FIRST_GATHER = 2
MAP_STEP = 4
SPREAD = 1
W2_STEP = 6
REGROUP_LAG = 2
PAIRS = 2 * HIDDEN_PASSES
PAIRS_AHEAD = 4

FLOPS = 2 * BATCH * MAP * HIDDEN * (8 * CHANNELS + CHANNELS)


def window_position(u, t):
    return 5 * (t // 2) + 2 * u + t % 2


def pixel_shift(u, t):
    position = window_position(u, t)
    return SIDE * (position // 3 - 1) + (position % 3 - 1)


def regroup(grouped, planes, copy):
    copy(
        out=grouped.rearrange("p (x i) t -> p x t i", i=RUN),
        in_=planes.rearrange("p t (x i) -> p x t i", i=RUN),
    )


def tile_localpredictor_pa_kernel(tc, z, W1, b1, W2, b2, out):
    nc = tc.nc
    z_maps = z.rearrange("b c h w -> b c (h w)")
    out_maps = out.rearrange("b k h w -> b k (h w)")
    w1_rows = W1.rearrange("(s m t) k -> s m t k", m=P, t=PACK)

    with ExitStack() as ctx:
        ctx.enter_context(tc.manual_schedule())
        keep = ctx.enter_context(tc.tile_pool(name="keep", bufs=1))
        w1_pool = ctx.enter_context(tc.tile_pool(name="w1_pool", bufs=PAIRS))
        stage = ctx.enter_context(tc.tile_pool(name="stage", bufs=4))
        shift_pool = ctx.enter_context(tc.tile_pool(name="shift_pool", bufs=2 * CHANNEL_PASSES))
        win_pool = ctx.enter_context(tc.tile_pool(name="win_pool", bufs=2))
        h_pool = ctx.enter_context(tc.tile_pool(name="h_pool", bufs=5))
        psum = ctx.enter_context(tc.psum_pool(name="psum", bufs=6))
        psum_out = ctx.enter_context(tc.psum_pool(name="psum_out", bufs=2))

        identity = keep.tile([P, P], F32, name="identity")
        make_identity(nc, identity[:])
        table_loaded = keep.tile([P, 1], F32, name="table_loaded")
        nc.scalar.activation(out=table_loaded[:], in_=identity[:, 0:1], func=ACT.Relu)

        w1_raw_tiles = {}

        def load_w1(q):
            w1_raw = w1_pool.tile([P, 2, CHANNELS * WINDOW], BF16, name="w1_raw")
            s, pair = divmod(q, 2)
            nc.sync.dma_start(out=w1_raw[:], in_=w1_rows[s, :, 2 * pair : 2 * pair + 2, :])
            w1_raw_tiles[q] = w1_raw

        def dropped_column(t):
            return (SIDE - 1, None, 0)[window_position(0, t) % 3]

        moved = {}

        def clear_gaps(b):
            moved[b] = keep.tile([P, PACK, BASE + MAP + BASE], BF16, name="moved%d" % b)

            nc.vector.memset(moved[b][:, :, 0 : BASE + 2 * SIDE], 0.0)
            nc.vector.memset(moved[b][:, :, BASE + MAP - 2 * SIDE :], 0.0)
            for t in range(PACK):
                if dropped_column(t) is not None:
                    first = BASE - pixel_shift(0, t)
                    nc.vector.memset(moved[b][:, t, first + dropped_column(t) : first + MAP : SIDE], 0.0)

        for b in range(BATCH):
            clear_gaps(b)
        z_rows = {}

        def copy_rows(b, t):
            first = BASE - pixel_shift(0, t)
            return moved[b][:, t, first : first + MAP].rearrange("c (i j) -> c i j", j=SIDE)

        def load_map(b):
            if b == 0:
                z_rows[b] = keep.tile([P, SIDE, SIDE], BF16, name="z_rows")[:]
            else:
                z_rows[b] = copy_rows(b, WHOLE)
            for g in range(CHANNEL_PASSES):
                nc.sync.dma_start(
                    out=z_rows[b][g:P:2].rearrange("c i j -> c (i j)"),
                    in_=z_maps[b, PASS_CHANNELS * g : PASS_CHANNELS * (g + 1)],
                )

        def move_map(b):
            for t in range(PACK):
                rows = copy_rows(b, t)
                if t == WHOLE:
                    if b == 0:
                        nc.scalar.copy(out=rows, in_=z_rows[b])
                else:
                    kept = slice(1, SIDE) if dropped_column(t) == 0 else slice(0, SIDE - 1)
                    nc.vector.tensor_copy(out=rows[:, :, kept], in_=z_rows[b][:, :, kept])

        shifted = {}

        def load_shifted(n, g):
            b, half = divmod(n, TILES_PER_MAP)
            shifted[n, g] = shift_pool.tile([P, PACK, PIXEL_TILE], BF16, name="shifted_maps")
            for u, values, source, rows in MOVES:
                first = BASE + PIXEL_TILE * half + SIDE * rows
                nc.sync.dma_start(
                    out=shifted[n, g][u:P:2, values],
                    in_=moved[b][g:P:2, source, first : first + PIXEL_TILE],
                )

        bias1 = keep.tile([P, HIDDEN_PASSES, PACK], BF16, name="bias1")
        nc.scalar.dma_start(out=bias1[:], in_=b1.rearrange("(s m t) -> m s t", m=P, t=PACK))
        bias2 = keep.tile([P, 1], BF16, name="bias2")
        nc.scalar.dma_start(out=bias2[:], in_=b2.rearrange("(k o) -> k o", o=1))
        load_map(0)
        for q in range(AHEAD):
            load_w1(q)
        move_map(0)
        for g in range(CHANNEL_PASSES):
            load_shifted(0, g)
        for q in range(AHEAD, PAIRS):
            load_w1(q)
        for g in range(CHANNEL_PASSES):
            load_shifted(1, g)
        w2_rows = keep.tile([P, HIDDEN], BF16, name="w2_rows")
        nc.sync.dma_start(out=w2_rows[:], in_=W2)

        def load_second_map():
            move_map(1)
            for n in range(TILES_PER_MAP, PIXEL_TILES):
                for g in range(CHANNEL_PASSES):
                    load_shifted(n, g)

        w1_codes = keep.tile([P, 2 * HIDDEN_PASSES, CHANNEL_PASSES, 2 * P], U32, name="w1_codes", align_bytes=64)
        w1_scales = keep.tile([P, 2 * HIDDEN_PASSES, CHANNEL_PASSES, 2 * P], U8, name="w1_scales", align_bytes=64)

        def compact_w1(q):
            halves = stage.tile([P, 2, 2, K_PASS], BF16, name="halves")
            by_channel = w1_raw_tiles[q][:].rearrange("m j (c x) -> m j c x", x=WINDOW)
            for a in range(2):
                nc.vector.tensor_copy(
                    out=halves[:, a].rearrange("m j (c r) -> m j c r", r=PACK),
                    in_=by_channel[:, :, :, 5 * a : 5 * a + PACK],
                )
            return halves

        def transpose_w1(halves):
            words = halves[:].bitcast(F32)
            w1_grouped = stage.tile([P, CHANNEL_PASSES, 2 * P, 2], F32, name="w1_grouped", align_bytes=64)
            for g in range(CHANNEL_PASSES):
                bank = psum.tile([P, 2, 2, P], F32, tag="bank")
                for a in range(2):
                    for j in range(2):
                        nc.tensor.transpose(bank[:, a, j, :], words[:, a, j, P * g : P * (g + 1)], identity[:])
                nc.scalar.copy(out=w1_grouped[:, g], in_=bank[:].rearrange("p a j m -> p (j m) a"))
            return w1_grouped

        def quantise_w1(q, w1_grouped):
            nc.vector.quantize_mx(
                out=w1_codes[:, q].rearrange("p g m -> p (g m)").bitcast(FP8X4),
                scales=w1_scales[:, q].rearrange("p g m -> p (g m)"),
                in_=w1_grouped[:].rearrange("p g m a -> p (g m a)").bitcast(BF16),
            )

        w2_codes = keep.tile([P, HIDDEN_PASSES, P], U32, name="w2_codes", align_bytes=64)
        w2_scales = keep.tile([P, HIDDEN_PASSES, P], U8, name="w2_scales", align_bytes=64)

        w2_words = keep.tile([P, HIDDEN_PASSES, 2, P], F32, name="w2_words")

        def part_w2():
            nc.vector.tensor_copy(
                out=w2_words[:], in_=w2_rows[:].bitcast(F32).rearrange("k (h p u) -> k h u p", h=HIDDEN_PASSES, u=2)
            )

        def prepare_w2():
            words = w2_words[:]
            w2_grouped = keep.tile([P, HIDDEN_PASSES * P, 2], F32, name="w2_grouped", align_bytes=64)
            for pair in range(HIDDEN_PASSES // 2):
                bank = psum.tile([P, 2, 2, P], F32, tag="bank")
                for u in range(2):
                    for j in range(2):
                        s = 2 * pair + j
                        nc.tensor.transpose(bank[:, u, j, :], words[:, s, u, :], identity[:])
                nc.scalar.copy(
                    out=w2_grouped[:, 2 * P * pair : 2 * P * (pair + 1), :],
                    in_=bank[:].rearrange("p u j k -> p (j k) u"),
                )
            nc.vector.quantize_mx(
                out=w2_codes[:].rearrange("p s k -> p (s k)").bitcast(FP8X4),
                scales=w2_scales[:].rearrange("p s k -> p (s k)"),
                in_=w2_grouped[:].rearrange("p k u -> p (k u)").bitcast(BF16),
            )

        win_operands = {}

        def start_windows(n):
            win_grouped = win_pool.tile([P, CHANNEL_PASSES, PIXEL_TILE, PACK], BF16, name="win_grouped", align_bytes=64)
            win_codes = win_pool.tile([P, CHANNEL_PASSES, PIXEL_TILE], U32, name="win_codes", align_bytes=64)
            win_scales = win_pool.tile([P, CHANNEL_PASSES, PIXEL_TILE], U8, name="win_scales", align_bytes=64)
            win_operands[n] = (win_codes, win_scales)
            return win_grouped

        def gather_windows(n, g, win_grouped, columns=slice(0, PIXEL_TILE), copy=nc.vector.tensor_copy):
            regroup(win_grouped[:, g, columns], shifted[n, g][:, :, columns], copy)

        def quantise_windows(n, g_first, g_end, win_grouped):
            win_codes, win_scales = win_operands[n]
            nc.vector.quantize_mx(
                out=win_codes[:, g_first:g_end].rearrange("p g x -> p (g x)").bitcast(FP8X4),
                scales=win_scales[:, g_first:g_end].rearrange("p g x -> p (g x)"),
                in_=win_grouped[:, g_first:g_end].rearrange("p g x t -> p (g x t)"),
            )

        def pieces(count):
            width = PIXEL_TILE // count
            return [slice(width * piece, width * (piece + 1)) for piece in range(count)]

        blocks = [(n, s, columns) for n in range(PIXEL_TILES) for s in range(HIDDEN_PASSES) for columns in pieces(1)]
        last_tile, last_pass, whole = blocks.pop()
        blocks.extend((last_tile, last_pass, columns) for columns in pieces(TAIL_PIECES))

        hidden_blocks = {}

        def first_layer(i, pair, order):
            n, s, columns = blocks[i]
            width = columns.stop - columns.start
            if pair == 0:
                hidden_blocks[i] = h_pool.tile([P, PACK, width], BF16, name="hidden", bufs=HIDDEN_BUFS)
            win_codes, win_scales = win_operands[n]
            banks = {}
            for j, g in order:
                q, t = 2 * s + pair, 2 * pair + j
                if g == 0:
                    banks[j] = psum.tile([P, width], F32, name="hidden_bank", tag="bank")
                nc.tensor.matmul_mx(
                    out=banks[j][:],
                    lhsT=w1_codes[:, q, g, P * j : P * (j + 1)].bitcast(FP8X4),
                    lhsT_scale=w1_scales[:, q, g, P * j : P * (j + 1)],
                    rhs=win_codes[:, g, columns].bitcast(FP8X4),
                    rhs_scale=win_scales[:, g, columns],
                    start=(g == 0),
                    stop=(g == CHANNEL_PASSES - 1),
                )
                if g == CHANNEL_PASSES - 1:
                    nc.scalar.activation(
                        out=hidden_blocks[i][:, t, :], in_=banks[j][:], func=ACT.Relu, bias=bias1[:, s, t : t + 1]
                    )

        grouped_blocks = {}
        quantised_blocks = {}

        def regroup_hidden(i):
            width = hidden_blocks[i].shape[2]
            grouped_blocks[i] = h_pool.tile([P, width, PACK], BF16, name="h_grouped", align_bytes=64, bufs=4)
            regroup(grouped_blocks[i][:], hidden_blocks[i][:], nc.vector.tensor_copy)

        def quantise_hidden(i):
            width = hidden_blocks[i].shape[2]
            h_codes = h_pool.tile([P, width], U32, name="h_codes", align_bytes=64)
            h_scales = h_pool.tile([P, width], U8, name="h_scales", align_bytes=64)
            nc.vector.quantize_mx(
                out=h_codes[:].bitcast(FP8X4),
                scales=h_scales[:],
                in_=grouped_blocks[i][:].rearrange("p x t -> p (x t)"),
            )
            quantised_blocks[i] = (h_codes, h_scales)

        out_banks = {}

        def second_layer(i):
            n, s, columns = blocks[i]
            codes, scales = quantised_blocks[i]
            for piece in pieces(TAIL_PIECES if n == last_tile else 1):
                if not columns.start <= piece.start < columns.stop:
                    continue
                width = piece.stop - piece.start
                own = slice(piece.start - columns.start, piece.stop - columns.start)
                if s == 0:
                    out_banks[n, piece.start] = psum_out.tile([P, width], F32, name="out_bank")
                out_bank = out_banks[n, piece.start]
                nc.tensor.matmul_mx(
                    out=out_bank[:],
                    lhsT=w2_codes[:, s, :].bitcast(FP8X4),
                    lhsT_scale=w2_scales[:, s, :],
                    rhs=codes[:, own].bitcast(FP8X4),
                    rhs_scale=scales[:, own],
                    start=(s == 0),
                    stop=(s == HIDDEN_PASSES - 1),
                )
                if s == HIDDEN_PASSES - 1:
                    b, half = divmod(n, TILES_PER_MAP)
                    result = stage.tile([P, width], F32, name="result")
                    nc.scalar.activation(out=result[:], in_=out_bank[:], func=ACT.Identity, bias=bias2[:, 0:1])
                    first = PIXEL_TILE * half + piece.start
                    nc.sync.dma_start(out=out_maps[b, :, first : first + width], in_=result[:])

        windows = {0: start_windows(0)}
        w1_grouped_tiles = {}
        halves = {}

        def compact(q):
            if q < PAIRS:
                halves[q] = compact_w1(q)

        def turn(q):
            if q < PAIRS:
                w1_grouped_tiles[q] = transpose_w1(halves[q])

        def quantise(q):
            if q < PAIRS:
                quantise_w1(q, w1_grouped_tiles[q])

        compact(0)
        turn(0)
        compact(1)
        turn(1)
        quantise(0)
        compact(2)
        turn(2)
        first_half, second_half = pieces(2)
        gather_windows(0, 1, windows[0], second_half, nc.scalar.copy)
        gather_windows(0, 0, windows[0])
        quantise(1)
        gather_windows(0, 1, windows[0], first_half)
        quantise_windows(0, 0, 1, windows[0])
        quantise(2)
        quantise_windows(0, 1, 2, windows[0])
        load_map(1)
        for q in range(AHEAD, AHEAD + RUN_PAIRS):
            compact(q)

        tile_major = [(j, g) for j in range(2) for g in range(CHANNEL_PASSES)]
        pass_major = [(j, g) for g in range(CHANNEL_PASSES) for j in range(2)]
        for h in range(2 * len(blocks) + OUTPUT_LAG):
            i, pair = divmod(h, 2)
            in_first = i < len(blocks)
            if in_first:
                first_layer(i, pair, pass_major if h == 0 else tile_major)
                n, s, columns = blocks[i]
            if h % RUN_PAIRS == 0:
                for q in range(h + AHEAD, h + AHEAD + RUN_PAIRS):
                    turn(q)
                for q in range(h + AHEAD + RUN_PAIRS, h + AHEAD + 2 * RUN_PAIRS):
                    compact(q)
            if h > 0:
                quantise(h + AHEAD - 1)
            for k in range(len(blocks)):
                quantise_step = 2 * k + REGROUP_LAG + (1 if k >= len(blocks) - FLUSHED else QUANT_LAG)
                if h == 2 * k + REGROUP_LAG:
                    regroup_hidden(k)
                if h == quantise_step:
                    quantise_hidden(k)
            if in_first and n + 1 < PIXEL_TILES:
                r = 2 * s + pair
                f = FIRST_GATHER if n == 0 else GATHER_STEP
                if r == f:
                    windows[n + 1] = start_windows(n + 1)
                    gather_windows(n + 1, 0, windows[n + 1])
                if r == f + SPREAD:
                    gather_windows(n + 1, 1, windows[n + 1])
                if r == f + 2 * SPREAD:
                    quantise_windows(n + 1, 0, CHANNEL_PASSES, windows[n + 1])
            if h == W2_STEP - PART_LAG:
                part_w2()
            if h == W2_STEP:
                prepare_w2()
            if h == MAP_STEP:
                load_second_map()
            k = (h - OUTPUT_LAG) // 2
            if 0 <= k < len(blocks) and (h - OUTPUT_LAG) % 2 == 1:
                second_layer(k)
